import numpy as np
import ml_dtypes


def mxq(x, axis, fmt="e4m3"):
    dtype, down = {"e4m3": (ml_dtypes.float8_e4m3fn, 7), "e5m2": (ml_dtypes.float8_e5m2, 14)}[fmt]
    v = np.moveaxis(np.asarray(x, np.float32).astype(ml_dtypes.bfloat16).astype(np.float64), axis, -1)
    blocks = v.reshape(v.shape[:-1] + (-1, 32))
    amax = np.abs(blocks).max(-1, keepdims=True)
    byte = np.maximum(np.where(amax > 0, np.frexp(amax)[1] - 1 + 127, 0) - down, 1)
    scale = np.exp2(byte - 127.0)
    codes = (blocks / scale).astype(np.float32).astype(dtype).astype(np.float64)
    return np.moveaxis((codes * scale).reshape(v.shape), -1, axis)


WIDE = False


def mx_kscale(k):
    if not WIDE:
        return np.ones(k)
    levels = np.array([10, -10, 5, -5, 0])
    if k % 512:
        return np.exp2(np.random.permutation(np.resize(levels, k // 32))).repeat(32)
    a = np.empty((k // 512, 16))
    for p in range(k // 512):
        a[p, :8] = np.random.permutation(np.resize(levels, 8))
        for g in range(8):
            far = levels[np.abs(levels - a[p, g]) >= 10]
            a[p, g + 8] = far[np.random.randint(len(far))]
    return np.exp2(a.ravel()).repeat(32)


BF16 = ml_dtypes.bfloat16


def bf(x):
    return np.asarray(x, np.float32).astype(BF16)


def f64(x):
    return np.asarray(x).astype(np.float64)


B, S, DIM, H, DH, DV, R = 2, 2048, 512, 4, 128, 128, 512
EPS = 1e-6
N = H * (DH + DV)


def rmsnorm(c, w):
    norm = np.mean(c * c, axis=-1, keepdims=True)
    return w * (c * (1.0 / np.sqrt(norm + EPS)))


def setup_inputs():
    s, t = mx_kscale(DIM), mx_kscale(R)
    return {"x": bf(np.random.standard_normal((B, S, DIM)) * s),
            "wkv_a_w": bf(np.random.standard_normal((R, DIM)) / np.sqrt(DIM) / s[None, :]),
            "wkv_a_b": bf(np.random.standard_normal(R) * 0.3),
            "kv_norm_w": bf((1.0 + 0.1 * np.random.standard_normal(R)) * t),
            "wkv_b_w": bf(np.random.standard_normal((N, R)) / np.sqrt(R) / t[None, :]),
            "wkv_b_b": bf(np.random.standard_normal(N) * 0.3)}


def reference(x, wkv_a_w, wkv_a_b, kv_norm_w, wkv_b_w, wkv_b_b):
    c = (mxq(f64(x), 2, "e4m3") @ mxq(f64(wkv_a_w), 1, "e4m3").T) + f64(wkv_a_b)
    kv_c = rmsnorm(c, f64(kv_norm_w))
    kv = (mxq(kv_c, 2, "e4m3") @ mxq(f64(wkv_b_w), 1, "e4m3").T) + f64(wkv_b_b)
    kv = kv.reshape(B, S, H, DH + DV)
    return kv[..., :DH], kv[..., DH:]

@@ -1,0 +1,311 @@
+from contextlib import ExitStack
+
+import concourse.mybir as mybir
+from concourse.masks import make_identity
+
+F32 = mybir.dt.float32
+BF16 = mybir.dt.bfloat16
+U32 = mybir.dt.uint32
+U8 = mybir.dt.uint8
+FP8X4 = mybir.dt.float8_e4m3fn_x4
+ADD = mybir.AluOpType.add
+MULT = mybir.AluOpType.mult
+ACT = mybir.ActivationFunctionType
+
+P = 128
+PACK = 4
+HALVES = 2
+TOKENS = 4096
+K = 512
+HEADS = 4
+HEAD = 128
+KV = 2
+EPS = 1e-6
+
+GROUP_TILES = 4
+GROUPS = TOKENS // (P * GROUP_TILES)
+ROUND_TILES = 2
+ROUNDS = TOKENS // (P * ROUND_TILES)
+ROUND_COLS = ROUND_TILES * P
+
+BIAS_A = 0
+GAIN = K
+BIAS_B = 2 * K
+VECTOR_COLS = 2 * K + HEADS * KV * HEAD
+
+FLOPS = 2 * TOKENS * K * K + 2 * TOKENS * K * (HEADS * KV * HEAD)
+
+
+def block(i, width):
+    return slice(i * width, (i + 1) * width)
+
+
+def live(r):
+    return 0 <= r < ROUNDS
+
+
+def tile_mla_pa_t_kernel(
+    tc, x, wkv_a_w, wkv_a_b, kv_norm_w, wkv_b_w, wkv_b_b, out_0, out_1
+):
+    nc = tc.nc
+    x_groups = x.flatten_outer_dims().rearrange("(g p i) d -> g p (i d)", p=P, i=GROUP_TILES)
+    out_groups = [
+        o.rearrange("b s h c -> (b s) (h c)").rearrange("(g p i) n -> g p i n", p=P, i=GROUP_TILES)
+        for o in (out_0, out_1)
+    ]
+
+    with ExitStack() as stack:
+        keep = stack.enter_context(tc.tile_pool(name="keep", bufs=1))
+        work = stack.enter_context(tc.tile_pool(name="work", bufs=2))
+        scrap = stack.enter_context(tc.tile_pool(name="scrap", bufs=4))
+        stage = stack.enter_context(tc.tile_pool(name="stage", bufs=4))
+        psum_t = stack.enter_context(tc.psum_pool(name="psum_t", bufs=1))
+        psum_c = stack.enter_context(tc.psum_pool(name="psum_c", bufs=ROUND_TILES))
+        psum_o = stack.enter_context(tc.psum_pool(name="psum_o", bufs=ROUND_TILES * KV))
+        stack.enter_context(tc.manual_schedule())
+
+        vectors = keep.tile([P, VECTOR_COLS], BF16)
+        nc.vector.memset(vectors[:], 0.0)
+        for first, vector in ((BIAS_A, wkv_a_b), (GAIN, kv_norm_w), (BIAS_B, wkv_b_b)):
+            nc.sync.dma_start(
+                out=vectors[0:1, first : first + vector.shape[0]],
+                in_=vector.rearrange("(o n) -> o n", o=1),
+            )
+        wa_sb = keep.tile([P, K // P, K], BF16)
+        wb_sb = keep.tile([P, HEADS, KV, K], BF16)
+        x_sb = keep.tile([P, GROUPS, GROUP_TILES * K], BF16)
+        nc.sync.dma_start(out=wa_sb[:], in_=wkv_a_w.rearrange("(m p) d -> p m d", p=P))
+        nc.sync.dma_start(out=x_sb[:, 0, :], in_=x_groups[0])
+        wb_heads = wkv_b_w.rearrange("(h s p) r -> h p s r", s=KV, p=P)
+        for h in range(HEADS):
+            nc.sync.dma_start(out=wb_sb[:, h], in_=wb_heads[h])
+        for g in range(1, GROUPS):
+            nc.sync.dma_start(out=x_sb[:, g, :], in_=x_groups[g])
+
+        ident = keep.tile([P, P], F32)
+        make_identity(nc, ident[:])
+        one = keep.tile([P, 1], F32)
+        nc.vector.memset(one[:], 1.0)
+        nc.scalar.activation(out=one[:], in_=one[:], func=ACT.Sqrt)
+        eps = keep.tile([P, 1], F32)
+        nc.vector.memset(eps[:], EPS)
+
+        ones = keep.tile([P, P], BF16)
+        nc.vector.memset(ones[:], 1.0)
+        spread = keep.tile([P, VECTOR_COLS], BF16)
+        for b in range(VECTOR_COLS // K):
+            spread_bank = psum_o.tile([P, K], F32, tag="o")
+            nc.tensor.matmul(
+                out=spread_bank[:], lhsT=ones[:], rhs=vectors[:, block(b, K)], start=True, stop=True
+            )
+            nc.vector.tensor_copy(out=spread[:, block(b, K)], in_=spread_bank[:])
+        bias_a = spread[:, BIAS_A : BIAS_A + K]
+        gain = spread[:, GAIN : GAIN + K]
+        bias_b = spread[:, BIAS_B:VECTOR_COLS].rearrange("p (h s c) -> p h s c", h=HEADS, s=KV)
+
+        def transpose_words(bank, rows):
+            for s in range(len(rows)):
+                words = rows[s].bitcast(F32)
+                for u in range(HALVES):
+                    nc.tensor.transpose(bank[:, s, u, :], words[:, u :: HALVES], ident[:])
+
+        def pair_halves(bank):
+            return bank[:].rearrange("p s u r -> p s r u")
+
+        wa_grouped = keep.tile([P, K, PACK], BF16, align_bytes=64)
+        wa_codes = keep.tile([P, K], U32, align_bytes=64)
+        wa_scales = keep.tile([P, K], U8, align_bytes=64)
+        for b in range(2):
+            wa_bank = psum_o.tile([P, 2, HALVES, P], F32, tag="o")
+            transpose_words(wa_bank, [wa_sb[:, 2 * b + s, :] for s in range(2)])
+            nc.scalar.copy(
+                out=wa_grouped[:, block(b, 2 * P), :]
+                .bitcast(F32)
+                .rearrange("p (s r) u -> p s r u", s=2),
+                in_=pair_halves(wa_bank),
+            )
+        nc.vector.quantize_mx(
+            out=wa_codes[:].bitcast(FP8X4),
+            scales=wa_scales[:],
+            in_=wa_grouped[:].rearrange("p r j -> p (r j)"),
+        )
+
+        wb_codes = keep.tile([P, KV, HEADS, HEAD], U32, align_bytes=64)
+        wb_scales = keep.tile([P, KV, HEADS, HEAD], U8, align_bytes=64)
+        wb_banks = {}
+
+        def transpose_wb(h):
+            wb_banks[h] = psum_o.tile([P, KV, HALVES, P], F32, tag="o", name="wb_bank")
+            transpose_words(wb_banks[h], [wb_sb[:, h, s, :] for s in range(KV)])
+
+        def quantise_wb(h):
+            wb_grouped = work.tile([P, KV, HEAD, PACK], BF16, align_bytes=64)
+            nc.vector.tensor_copy(out=wb_grouped[:].bitcast(F32), in_=pair_halves(wb_banks[h]))
+            for s in range(KV):
+                nc.vector.quantize_mx(
+                    out=wb_codes[:, s, h, :].bitcast(FP8X4),
+                    scales=wb_scales[:, s, h, :],
+                    in_=wb_grouped[:, s].rearrange("p r j -> p (r j)"),
+                )
+
+        x_bank, x_grouped, x_codes, x_scales = {}, {}, {}, {}
+        c_bank, c_biased, c_gained, rstd = {}, {}, {}, {}
+        l_rows, l_bank, l_grouped, l_codes, l_scales = {}, {}, {}, {}, {}
+        o_bank = {}
+
+        def transpose_x(r):
+            g, first = divmod(r * ROUND_TILES, GROUP_TILES)
+            x_bank[r] = psum_t.tile([P, ROUND_TILES, HALVES, P], F32, name="x_bank")
+            transpose_words(
+                x_bank[r], [x_sb[:, g, block(first + s, K)] for s in range(ROUND_TILES)]
+            )
+
+        def regroup_x(r):
+            x_grouped[r] = work.tile(
+                [P, ROUND_TILES, P, PACK], BF16, align_bytes=64, name="x_grouped"
+            )
+            nc.scalar.copy(out=x_grouped[r][:].bitcast(F32), in_=pair_halves(x_bank[r]))
+
+        def quantise(grouped, codes, scales):
+            nc.vector.quantize_mx(
+                out=codes[:].bitcast(FP8X4),
+                scales=scales[:],
+                in_=grouped[:].rearrange("p s t j -> p (s t j)"),
+            )
+
+        def quantise_x(r):
+            x_codes[r] = work.tile([P, ROUND_COLS], U32, align_bytes=64, name="x_codes")
+            x_scales[r] = work.tile([P, ROUND_COLS], U8, align_bytes=64, name="x_scales")
+            quantise(x_grouped[r], x_codes[r], x_scales[r])
+
+        def first_matmul(r):
+            for s in range(ROUND_TILES):
+                c_bank[r, s] = psum_c.tile([P, K], F32, name="c_bank")
+                nc.tensor.matmul_mx(
+                    out=c_bank[r, s][:],
+                    lhsT=x_codes[r][:, block(s, P)].bitcast(FP8X4),
+                    lhsT_scale=x_scales[r][:, block(s, P)],
+                    rhs=wa_codes[:].bitcast(FP8X4),
+                    rhs_scale=wa_scales[:],
+                    start=True,
+                    stop=True,
+                )
+
+        def add_first_bias(r):
+            c_biased[r] = work.tile([P, ROUND_TILES, K], F32, name="c_biased")
+            for s in range(ROUND_TILES):
+                nc.vector.tensor_tensor(
+                    out=c_biased[r][:, s, :], in0=c_bank[r, s][:], in1=bias_a, op=ADD
+                )
+
+        def apply_gain(r):
+            c_gained[r] = work.tile([P, ROUND_TILES, K], F32, name="c_gained")
+            for s in range(ROUND_TILES):
+                nc.gpsimd.tensor_tensor(
+                    out=c_gained[r][:, s, :], in0=c_biased[r][:, s, :], in1=gain, op=MULT
+                )
+
+        def root_mean_square(r):
+            sum_sq = work.tile([P, ROUND_TILES], F32, name="sum_sq")
+            for s in range(ROUND_TILES):
+                squares = scrap.tile([P, K], BF16, name="squares")
+                nc.scalar.activation(
+                    out=squares[:],
+                    in_=c_biased[r][:, s, :],
+                    func=ACT.Square,
+                    accum_out=sum_sq[:, s : s + 1],
+                )
+            rms = work.tile([P, ROUND_TILES], F32, name="rms")
+            nc.scalar.activation(
+                out=rms[:], in_=sum_sq[:], func=ACT.Sqrt, scale=1.0 / K, bias=eps[:]
+            )
+            return rms
+
+        def invert(r, rms):
+            rstd[r] = work.tile([P, ROUND_TILES], F32, name="rstd")
+            nc.vector.reciprocal(out=rstd[r][:], in_=rms[:])
+
+        def normalise(r):
+            l_rows[r] = work.tile([P, ROUND_TILES, K], BF16, name="l_rows")
+            for s in range(ROUND_TILES):
+                nc.scalar.activation(
+                    out=l_rows[r][:, s, :],
+                    in_=c_gained[r][:, s, :],
+                    func=ACT.Copy,
+                    scale=rstd[r][:, s : s + 1],
+                )
+
+        def transpose_latent(r):
+            l_bank[r] = psum_t.tile([P, ROUND_TILES, HALVES, P], F32, name="l_bank")
+            transpose_words(l_bank[r], [l_rows[r][:, s, :] for s in range(ROUND_TILES)])
+
+        def regroup_latent(r):
+            l_grouped[r] = work.tile(
+                [P, ROUND_TILES, P, PACK], BF16, align_bytes=64, name="l_grouped"
+            )
+            nc.scalar.copy(out=l_grouped[r][:].bitcast(F32), in_=pair_halves(l_bank[r]))
+
+        def quantise_latent(r):
+            l_codes[r] = work.tile([P, ROUND_COLS], U32, align_bytes=64, name="l_codes")
+            l_scales[r] = work.tile([P, ROUND_COLS], U8, align_bytes=64, name="l_scales")
+            quantise(l_grouped[r], l_codes[r], l_scales[r])
+
+        def second_matmul(r):
+            for kv in range(KV):
+                for s in range(ROUND_TILES):
+                    o_bank[r, s, kv] = psum_o.tile([P, HEADS, HEAD], F32, tag="o", name="o_bank")
+                    nc.tensor.matmul_mx(
+                        out=o_bank[r, s, kv][:].rearrange("p h c -> p (h c)"),
+                        lhsT=l_codes[r][:, block(s, P)].bitcast(FP8X4),
+                        lhsT_scale=l_scales[r][:, block(s, P)],
+                        rhs=wb_codes[:, kv].rearrange("p h c -> p (h c)").bitcast(FP8X4),
+                        rhs_scale=wb_scales[:, kv].rearrange("p h c -> p (h c)"),
+                        start=True,
+                        stop=True,
+                    )
+
+        def add_second_bias_and_store(r):
+            g, first = divmod(r * ROUND_TILES, GROUP_TILES)
+            result = stage.tile([P, KV, ROUND_TILES, HEADS, HEAD], F32, name="result")
+            for kv in range(KV):
+                for s in range(ROUND_TILES):
+                    nc.vector.tensor_tensor(
+                        out=result[:, kv, s], in0=o_bank[r, s, kv][:], in1=bias_b[:, :, kv, :], op=ADD
+                    )
+                nc.sync.dma_start(
+                    out=out_groups[kv][g][:, first : first + ROUND_TILES, :],
+                    in_=result[:, kv].rearrange("p s h c -> p s (h c)"),
+                )
+
+        X_AHEAD = 3
+        for n in range(-X_AHEAD, ROUNDS + 2):
+            if live(n):
+                add_first_bias(n)
+            if live(n - 1):
+                normalise(n - 1)
+            if live(n - 2):
+                second_matmul(n - 2)
+            if live(n + 1):
+                first_matmul(n + 1)
+            if live(n - 1):
+                transpose_latent(n - 1)
+            if live(n + X_AHEAD):
+                transpose_x(n + X_AHEAD)
+            if n + X_AHEAD < HEADS:
+                transpose_wb(n + X_AHEAD)
+            if live(n):
+                apply_gain(n)
+            if live(n - 2):
+                add_second_bias_and_store(n - 2)
+            if 0 <= n + 2 < HEADS:
+                quantise_wb(n + 2)
+            if live(n):
+                invert(n, root_mean_square(n))
+            if live(n - 1):
+                regroup_latent(n - 1)
+            if live(n + X_AHEAD):
+                regroup_x(n + X_AHEAD)
+            if live(n + 2):
+                quantise_x(n + 2)
+            if live(n - 1):
+                quantise_latent(n - 1)

@@ -11,10 +11,11 @@ FP8X4 = mybir.dt.float8_e4m3fn_x4
 ADD = mybir.AluOpType.add
 MULT = mybir.AluOpType.mult
 ACT = mybir.ActivationFunctionType
+AXIS_X = mybir.AxisListType.X
 
 P = 128
 PACK = 4
-HALVES = 2
+WORDS = 2
 TOKENS = 4096
 K = 512
 HEADS = 4
@@ -26,12 +27,8 @@ GROUP_TILES = 4
 GROUPS = TOKENS // (P * GROUP_TILES)
 ROUND_TILES = 2
 ROUNDS = TOKENS // (P * ROUND_TILES)
-ROUND_COLS = ROUND_TILES * P
-
-BIAS_A = 0
-GAIN = K
-BIAS_B = 2 * K
-VECTOR_COLS = 2 * K + HEADS * KV * HEAD
+COLS = ROUND_TILES * P
+G_COLS = 192
 
 FLOPS = 2 * TOKENS * K * K + 2 * TOKENS * K * (HEADS * KV * HEAD)
 
@@ -42,6 +39,18 @@ def block(i, width):
 
 def live(r):
     return 0 <= r < ROUNDS
+
+
+def regroup_on_vector(r):
+    return False
+
+
+def gain_on_vector(r):
+    return r < 2
+
+
+def gpsimd_cols(r):
+    return 0 if r < 2 else 192
 
 
 def tile_mla_pa_t_kernel(
@@ -56,26 +65,26 @@ def tile_mla_pa_t_kernel(
 
     with ExitStack() as stack:
         keep = stack.enter_context(tc.tile_pool(name="keep", bufs=1))
-        work = stack.enter_context(tc.tile_pool(name="work", bufs=2))
-        scrap = stack.enter_context(tc.tile_pool(name="scrap", bufs=4))
+        work = stack.enter_context(tc.tile_pool(name="work", bufs=4))
+        single = stack.enter_context(tc.tile_pool(name="single", bufs=1))
         stage = stack.enter_context(tc.tile_pool(name="stage", bufs=4))
-        psum_t = stack.enter_context(tc.psum_pool(name="psum_t", bufs=1))
-        psum_c = stack.enter_context(tc.psum_pool(name="psum_c", bufs=ROUND_TILES))
-        psum_o = stack.enter_context(tc.psum_pool(name="psum_o", bufs=ROUND_TILES * KV))
+        psum_c = stack.enter_context(tc.psum_pool(name="psum_c", bufs=1))
+        psum_s = stack.enter_context(tc.psum_pool(name="psum_s", bufs=1))
+        psum_o = stack.enter_context(tc.psum_pool(name="psum_o", bufs=4))
         stack.enter_context(tc.manual_schedule())
 
-        vectors = keep.tile([P, VECTOR_COLS], BF16)
-        nc.vector.memset(vectors[:], 0.0)
-        for first, vector in ((BIAS_A, wkv_a_b), (GAIN, kv_norm_w), (BIAS_B, wkv_b_b)):
-            nc.sync.dma_start(
-                out=vectors[0:1, first : first + vector.shape[0]],
-                in_=vector.rearrange("(o n) -> o n", o=1),
-            )
-        wa_sb = keep.tile([P, K // P, K], BF16)
+        bias_b_row = keep.tile([P, HEADS * KV * HEAD], BF16)
+        nc.vector.memset(bias_b_row[:], 0.0)
+        bias_a_bf = keep.tile([P, PACK], BF16)
+        gain_bf = keep.tile([P, PACK], BF16)
+        wa_sb = keep.tile([P, PACK, K], BF16)
         wb_sb = keep.tile([P, HEADS, KV, K], BF16)
         x_sb = keep.tile([P, GROUPS, GROUP_TILES * K], BF16)
-        nc.sync.dma_start(out=wa_sb[:], in_=wkv_a_w.rearrange("(m p) d -> p m d", p=P))
+        nc.sync.dma_start(out=wa_sb[:], in_=wkv_a_w.rearrange("(p j) d -> p j d", j=PACK))
         nc.sync.dma_start(out=x_sb[:, 0, :], in_=x_groups[0])
+        nc.scalar.dma_start(out=bias_a_bf[:], in_=wkv_a_b.rearrange("(p j) -> p j", j=PACK))
+        nc.scalar.dma_start(out=gain_bf[:], in_=kv_norm_w.rearrange("(p j) -> p j", j=PACK))
+        nc.scalar.dma_start(out=bias_b_row[0:1, :], in_=wkv_b_b.rearrange("(o n) -> o n", o=1))
         wb_heads = wkv_b_w.rearrange("(h s p) r -> h p s r", s=KV, p=P)
         for h in range(HEADS):
             nc.sync.dma_start(out=wb_sb[:, h], in_=wb_heads[h])
@@ -84,50 +93,48 @@ def tile_mla_pa_t_kernel(
 
         ident = keep.tile([P, P], F32)
         make_identity(nc, ident[:])
+        eps = keep.tile([P, 1], F32)
+        nc.vector.memset(eps[:], 0.0)
+        nc.vector.tensor_scalar(out=eps[:], in0=eps[:], scalar1=EPS, scalar2=None, op0=ADD)
         one = keep.tile([P, 1], F32)
         nc.vector.memset(one[:], 1.0)
-        nc.scalar.activation(out=one[:], in_=one[:], func=ACT.Sqrt)
-        eps = keep.tile([P, 1], F32)
-        nc.vector.memset(eps[:], EPS)
+        nc.scalar.activation(out=one[:], in_=one[:], func=ACT.Abs_reciprocal_sqrt)
+        ones_bf = keep.tile([P, P], BF16)
+        nc.vector.memset(ones_bf[:], 1.0)
 
-        ones = keep.tile([P, P], BF16)
-        nc.vector.memset(ones[:], 1.0)
-        spread = keep.tile([P, VECTOR_COLS], BF16)
-        for b in range(VECTOR_COLS // K):
-            spread_bank = psum_o.tile([P, K], F32, tag="o")
-            nc.tensor.matmul(
-                out=spread_bank[:], lhsT=ones[:], rhs=vectors[:, block(b, K)], start=True, stop=True
-            )
-            nc.vector.tensor_copy(out=spread[:, block(b, K)], in_=spread_bank[:])
-        bias_a = spread[:, BIAS_A : BIAS_A + K]
-        gain = spread[:, GAIN : GAIN + K]
-        bias_b = spread[:, BIAS_B:VECTOR_COLS].rearrange("p (h s c) -> p h s c", h=HEADS, s=KV)
+        bias_a = keep.tile([P, PACK], F32)
+        gain = keep.tile([P, PACK], F32)
+        gained_bias = keep.tile([P, PACK], F32)
+        nc.vector.tensor_copy(out=bias_a[:], in_=bias_a_bf[:])
+        nc.vector.tensor_copy(out=gain[:], in_=gain_bf[:])
+        nc.vector.tensor_tensor(out=gained_bias[:], in0=bias_a[:], in1=gain[:], op=MULT)
 
         def transpose_words(bank, rows):
             for s in range(len(rows)):
                 words = rows[s].bitcast(F32)
-                for u in range(HALVES):
-                    nc.tensor.transpose(bank[:, s, u, :], words[:, u :: HALVES], ident[:])
+                for u in range(WORDS):
+                    nc.tensor.transpose(bank[:, s, u, :], words[:, u::WORDS], ident[:])
 
-        def pair_halves(bank):
-            return bank[:].rearrange("p s u r -> p s r u")
+        def pair_words(bank):
+            return bank[:].rearrange("p s u m -> p s m u")
 
         wa_grouped = keep.tile([P, K, PACK], BF16, align_bytes=64)
         wa_codes = keep.tile([P, K], U32, align_bytes=64)
         wa_scales = keep.tile([P, K], U8, align_bytes=64)
         for b in range(2):
-            wa_bank = psum_o.tile([P, 2, HALVES, P], F32, tag="o")
+            wa_bank = psum_o.tile([P, 2, WORDS, P], F32, tag="o")
             transpose_words(wa_bank, [wa_sb[:, 2 * b + s, :] for s in range(2)])
-            nc.scalar.copy(
+            copy = nc.vector.tensor_copy if b == 1 else nc.scalar.copy
+            copy(
                 out=wa_grouped[:, block(b, 2 * P), :]
                 .bitcast(F32)
-                .rearrange("p (s r) u -> p s r u", s=2),
-                in_=pair_halves(wa_bank),
+                .rearrange("p (s m) u -> p s m u", s=2),
+                in_=pair_words(wa_bank),
             )
         nc.vector.quantize_mx(
             out=wa_codes[:].bitcast(FP8X4),
             scales=wa_scales[:],
-            in_=wa_grouped[:].rearrange("p r j -> p (r j)"),
+            in_=wa_grouped[:].rearrange("p m j -> p (m j)"),
         )
 
         wb_codes = keep.tile([P, KV, HEADS, HEAD], U32, align_bytes=64)
@@ -135,27 +142,42 @@ def tile_mla_pa_t_kernel(
         wb_banks = {}
 
         def transpose_wb(h):
-            wb_banks[h] = psum_o.tile([P, KV, HALVES, P], F32, tag="o", name="wb_bank")
+            wb_banks[h] = psum_o.tile([P, KV, WORDS, P], F32, tag="o", name="wb_bank")
             transpose_words(wb_banks[h], [wb_sb[:, h, s, :] for s in range(KV)])
 
+        wb_grouped = {}
+
+        def regroup_wb(h):
+            wb_grouped[h] = work.tile([P, KV, HEAD, PACK], BF16, align_bytes=64, name="wb_grouped")
+            nc.scalar.copy(out=wb_grouped[h][:].bitcast(F32), in_=pair_words(wb_banks[h]))
+
         def quantise_wb(h):
-            wb_grouped = work.tile([P, KV, HEAD, PACK], BF16, align_bytes=64)
-            nc.vector.tensor_copy(out=wb_grouped[:].bitcast(F32), in_=pair_halves(wb_banks[h]))
             for s in range(KV):
                 nc.vector.quantize_mx(
                     out=wb_codes[:, s, h, :].bitcast(FP8X4),
                     scales=wb_scales[:, s, h, :],
-                    in_=wb_grouped[:, s].rearrange("p r j -> p (r j)"),
+                    in_=wb_grouped[h][:, s].rearrange("p m j -> p (m j)"),
                 )
 
+        bias_b_all = keep.tile([P, HEADS, KV, HEAD], BF16)
+
+        def spread_bias_b():
+            flat = bias_b_all[:].rearrange("p h s c -> p (h s c)")
+            for b in range(KV):
+                bank = psum_o.tile([P, K], F32, tag="o", name="spread_bank")
+                nc.tensor.matmul(
+                    out=bank[:], lhsT=ones_bf[:], rhs=bias_b_row[:, block(b, K)], start=True, stop=True
+                )
+                nc.scalar.copy(out=flat[:, block(b, K)], in_=bank[:])
+
         x_bank, x_grouped, x_codes, x_scales = {}, {}, {}, {}
-        c_bank, c_biased, c_gained, rstd = {}, {}, {}, {}
-        l_rows, l_bank, l_grouped, l_codes, l_scales = {}, {}, {}, {}, {}
-        o_bank = {}
+        c_bank, y, squares, q_bank, rstd, factor_bank, factor = {}, {}, {}, {}, {}, {}, {}
+        l_grouped, l_codes, l_scales = {}, {}, {}
+        o_bank, result = {}, {}
 
         def transpose_x(r):
             g, first = divmod(r * ROUND_TILES, GROUP_TILES)
-            x_bank[r] = psum_t.tile([P, ROUND_TILES, HALVES, P], F32, name="x_bank")
+            x_bank[r] = psum_o.tile([P, ROUND_TILES, WORDS, P], F32, tag="o", name="x_bank")
             transpose_words(
                 x_bank[r], [x_sb[:, g, block(first + s, K)] for s in range(ROUND_TILES)]
             )
@@ -164,148 +186,248 @@ def tile_mla_pa_t_kernel(
             x_grouped[r] = work.tile(
                 [P, ROUND_TILES, P, PACK], BF16, align_bytes=64, name="x_grouped"
             )
-            nc.scalar.copy(out=x_grouped[r][:].bitcast(F32), in_=pair_halves(x_bank[r]))
-
-        def quantise(grouped, codes, scales):
-            nc.vector.quantize_mx(
-                out=codes[:].bitcast(FP8X4),
-                scales=scales[:],
-                in_=grouped[:].rearrange("p s t j -> p (s t j)"),
-            )
+            copy = nc.vector.tensor_copy if regroup_on_vector(r) else nc.scalar.copy
+            copy(out=x_grouped[r][:].bitcast(F32), in_=pair_words(x_bank[r]))
 
         def quantise_x(r):
-            x_codes[r] = work.tile([P, ROUND_COLS], U32, align_bytes=64, name="x_codes")
-            x_scales[r] = work.tile([P, ROUND_COLS], U8, align_bytes=64, name="x_scales")
-            quantise(x_grouped[r], x_codes[r], x_scales[r])
+            x_codes[r] = work.tile([P, COLS], U32, align_bytes=64, name="x_codes")
+            x_scales[r] = work.tile([P, COLS], U8, align_bytes=64, name="x_scales")
+            nc.vector.quantize_mx(
+                out=x_codes[r][:].bitcast(FP8X4),
+                scales=x_scales[r][:],
+                in_=x_grouped[r][:].rearrange("p s m j -> p (s m j)"),
+            )
 
-        def first_matmul(r):
-            for s in range(ROUND_TILES):
-                c_bank[r, s] = psum_c.tile([P, K], F32, name="c_bank")
+        def first_matmul(r, half):
+            c_bank[r, half] = psum_c.tile([P, 2, COLS], F32, tag="c%d" % half, name="c_bank")
+            for e in range(2):
+                j = 2 * half + e
                 nc.tensor.matmul_mx(
-                    out=c_bank[r, s][:],
-                    lhsT=x_codes[r][:, block(s, P)].bitcast(FP8X4),
-                    lhsT_scale=x_scales[r][:, block(s, P)],
-                    rhs=wa_codes[:].bitcast(FP8X4),
-                    rhs_scale=wa_scales[:],
+                    out=c_bank[r, half][:, e, :],
+                    lhsT=wa_codes[:, block(j, P)].bitcast(FP8X4),
+                    lhsT_scale=wa_scales[:, block(j, P)],
+                    rhs=x_codes[r][:].bitcast(FP8X4),
+                    rhs_scale=x_scales[r][:],
                     start=True,
                     stop=True,
                 )
 
-        def add_first_bias(r):
-            c_biased[r] = work.tile([P, ROUND_TILES, K], F32, name="c_biased")
-            for s in range(ROUND_TILES):
-                nc.vector.tensor_tensor(
-                    out=c_biased[r][:, s, :], in0=c_bank[r, s][:], in1=bias_a, op=ADD
-                )
-
-        def apply_gain(r):
-            c_gained[r] = work.tile([P, ROUND_TILES, K], F32, name="c_gained")
-            for s in range(ROUND_TILES):
-                nc.gpsimd.tensor_tensor(
-                    out=c_gained[r][:, s, :], in0=c_biased[r][:, s, :], in1=gain, op=MULT
-                )
-
-        def root_mean_square(r):
-            sum_sq = work.tile([P, ROUND_TILES], F32, name="sum_sq")
-            for s in range(ROUND_TILES):
-                squares = scrap.tile([P, K], BF16, name="squares")
+        def square(r, half):
+            if r not in squares:
+                squares[r] = work.tile([P, PACK, COLS], F32, name="squares")
+            for e in range(2):
+                j = 2 * half + e
                 nc.scalar.activation(
-                    out=squares[:],
-                    in_=c_biased[r][:, s, :],
+                    out=squares[r][:, j, :],
+                    in_=c_bank[r, half][:, e, :],
                     func=ACT.Square,
-                    accum_out=sum_sq[:, s : s + 1],
+                    bias=bias_a[:, j : j + 1],
                 )
-            rms = work.tile([P, ROUND_TILES], F32, name="rms")
-            nc.scalar.activation(
-                out=rms[:], in_=sum_sq[:], func=ACT.Sqrt, scale=1.0 / K, bias=eps[:]
-            )
-            return rms
 
-        def invert(r, rms):
-            rstd[r] = work.tile([P, ROUND_TILES], F32, name="rstd")
-            nc.vector.reciprocal(out=rstd[r][:], in_=rms[:])
+        def bias_and_gain(r, half):
+            if r not in y:
+                y[r] = work.tile([P, PACK, COLS], F32, name="y")
+            for e in range(2):
+                j = 2 * half + e
+                if gain_on_vector(r):
+                    nc.vector.tensor_scalar(
+                        out=y[r][:, j, :],
+                        in0=c_bank[r, half][:, e, :],
+                        scalar1=bias_a[:, j : j + 1],
+                        scalar2=gain[:, j : j + 1],
+                        op0=ADD,
+                        op1=MULT,
+                    )
+                else:
+                    nc.scalar.activation(
+                        out=y[r][:, j, :],
+                        in_=c_bank[r, half][:, e, :],
+                        func=ACT.Identity,
+                        scale=gain[:, j : j + 1],
+                        bias=gained_bias[:, j : j + 1],
+                    )
 
-        def normalise(r):
-            l_rows[r] = work.tile([P, ROUND_TILES, K], BF16, name="l_rows")
+        def add_squares(r):
+            q_bank[r] = psum_s.tile([P, ROUND_TILES, P], F32, tag="q", name="q_bank")
             for s in range(ROUND_TILES):
-                nc.scalar.activation(
-                    out=l_rows[r][:, s, :],
-                    in_=c_gained[r][:, s, :],
-                    func=ACT.Copy,
-                    scale=rstd[r][:, s : s + 1],
+                for j in range(PACK):
+                    nc.tensor.matmul(
+                        out=q_bank[r][:, s, :],
+                        lhsT=squares[r][:, j, block(s, P)],
+                        rhs=ident[:],
+                        is_transpose=True,
+                        start=(j == 0),
+                        stop=(j == PACK - 1),
+                    )
+
+        def inverse_root(r):
+            sum_sq = work.tile([P, ROUND_TILES], F32, name="sum_sq")
+            nc.vector.tensor_reduce(out=sum_sq[:], in_=q_bank[r][:], op=ADD, axis=AXIS_X)
+            rstd[r] = work.tile([P, ROUND_TILES], F32, name="rstd")
+            nc.scalar.activation(
+                out=rstd[r][:],
+                in_=sum_sq[:],
+                func=ACT.Abs_reciprocal_sqrt,
+                scale=1.0 / K,
+                bias=eps[:],
+            )
+
+        def spread_rstd(r):
+            factor_bank[r] = psum_s.tile([P, ROUND_TILES, P], F32, tag="f", name="factor_bank")
+            for s in range(ROUND_TILES):
+                nc.tensor.transpose(
+                    factor_bank[r][:, s, :],
+                    rstd[r][:, s : s + 1].to_broadcast([P, P]),
+                    ident[:],
                 )
 
-        def transpose_latent(r):
-            l_bank[r] = psum_t.tile([P, ROUND_TILES, HALVES, P], F32, name="l_bank")
-            transpose_words(l_bank[r], [l_rows[r][:, s, :] for s in range(ROUND_TILES)])
-
-        def regroup_latent(r):
-            l_grouped[r] = work.tile(
-                [P, ROUND_TILES, P, PACK], BF16, align_bytes=64, name="l_grouped"
+        def fetch_factor(r):
+            g = gpsimd_cols(r)
+            if g == 0:
+                return
+            factor[r] = work.tile([P, COLS], F32, name="factor")
+            nc.scalar.copy(
+                out=factor[r][:, 0:g], in_=factor_bank[r][:].rearrange("p s m -> p (s m)")[:, 0:g]
             )
-            nc.scalar.copy(out=l_grouped[r][:].bitcast(F32), in_=pair_halves(l_bank[r]))
+
+        def normalise(r, cols, engine, factors):
+            if r not in l_grouped:
+                l_grouped[r] = single.tile([P, COLS, PACK], BF16, align_bytes=64, name="l_grouped")
+            engine.tensor_tensor(
+                out=l_grouped[r][:, cols, :],
+                in0=y[r][:, :, cols].rearrange("p j m -> p m j"),
+                in1=factors.unsqueeze(2).to_broadcast([P, cols.stop - cols.start, PACK]),
+                op=MULT,
+            )
+
+        def normalise_gpsimd(r):
+            g = gpsimd_cols(r)
+            if g > 0:
+                normalise(r, slice(0, g), nc.gpsimd, factor[r][:, 0:g])
+
+        def normalise_vector(r):
+            g = gpsimd_cols(r)
+            if g < COLS:
+                cols = slice(g, COLS)
+                normalise(r, cols, nc.vector, factor_bank[r][:].rearrange("p s m -> p (s m)")[:, cols])
 
         def quantise_latent(r):
-            l_codes[r] = work.tile([P, ROUND_COLS], U32, align_bytes=64, name="l_codes")
-            l_scales[r] = work.tile([P, ROUND_COLS], U8, align_bytes=64, name="l_scales")
-            quantise(l_grouped[r], l_codes[r], l_scales[r])
+            l_codes[r] = work.tile([P, COLS], U32, align_bytes=64, name="l_codes")
+            l_scales[r] = work.tile([P, COLS], U8, align_bytes=64, name="l_scales")
+            nc.vector.quantize_mx(
+                out=l_codes[r][:].bitcast(FP8X4),
+                scales=l_scales[r][:],
+                in_=l_grouped[r][:].rearrange("p m j -> p (m j)"),
+            )
 
-        def second_matmul(r):
+        def second_matmul(r, s):
             for kv in range(KV):
-                for s in range(ROUND_TILES):
-                    o_bank[r, s, kv] = psum_o.tile([P, HEADS, HEAD], F32, tag="o", name="o_bank")
-                    nc.tensor.matmul_mx(
-                        out=o_bank[r, s, kv][:].rearrange("p h c -> p (h c)"),
-                        lhsT=l_codes[r][:, block(s, P)].bitcast(FP8X4),
-                        lhsT_scale=l_scales[r][:, block(s, P)],
-                        rhs=wb_codes[:, kv].rearrange("p h c -> p (h c)").bitcast(FP8X4),
-                        rhs_scale=wb_scales[:, kv].rearrange("p h c -> p (h c)"),
-                        start=True,
-                        stop=True,
-                    )
-
-        def add_second_bias_and_store(r):
-            g, first = divmod(r * ROUND_TILES, GROUP_TILES)
-            result = stage.tile([P, KV, ROUND_TILES, HEADS, HEAD], F32, name="result")
-            for kv in range(KV):
-                for s in range(ROUND_TILES):
-                    nc.vector.tensor_tensor(
-                        out=result[:, kv, s], in0=o_bank[r, s, kv][:], in1=bias_b[:, :, kv, :], op=ADD
-                    )
-                nc.sync.dma_start(
-                    out=out_groups[kv][g][:, first : first + ROUND_TILES, :],
-                    in_=result[:, kv].rearrange("p s h c -> p s (h c)"),
+                o_bank[r, s, kv] = psum_o.tile([P, HEADS, HEAD], F32, tag="o", name="o_bank")
+                nc.tensor.matmul_mx(
+                    out=o_bank[r, s, kv][:].rearrange("p h c -> p (h c)"),
+                    lhsT=l_codes[r][:, block(s, P)].bitcast(FP8X4),
+                    lhsT_scale=l_scales[r][:, block(s, P)],
+                    rhs=wb_codes[:, kv].rearrange("p h c -> p (h c)").bitcast(FP8X4),
+                    rhs_scale=wb_scales[:, kv].rearrange("p h c -> p (h c)"),
+                    start=True,
+                    stop=True,
                 )
 
-        X_AHEAD = 3
-        for n in range(-X_AHEAD, ROUNDS + 2):
-            if live(n):
-                add_first_bias(n)
-            if live(n - 1):
-                normalise(n - 1)
-            if live(n - 2):
-                second_matmul(n - 2)
-            if live(n + 1):
-                first_matmul(n + 1)
-            if live(n - 1):
-                transpose_latent(n - 1)
-            if live(n + X_AHEAD):
-                transpose_x(n + X_AHEAD)
-            if n + X_AHEAD < HEADS:
-                transpose_wb(n + X_AHEAD)
-            if live(n):
-                apply_gain(n)
-            if live(n - 2):
-                add_second_bias_and_store(n - 2)
-            if 0 <= n + 2 < HEADS:
-                quantise_wb(n + 2)
-            if live(n):
-                invert(n, root_mean_square(n))
-            if live(n - 1):
-                regroup_latent(n - 1)
-            if live(n + X_AHEAD):
-                regroup_x(n + X_AHEAD)
+        def add_second_bias(r, s, kv):
+            if s == 0 and kv == 0:
+                result[r] = stage.tile([P, KV, ROUND_TILES, HEADS, HEAD], F32, name="result")
+            nc.vector.tensor_tensor(
+                out=result[r][:, kv, s], in0=o_bank[r, s, kv][:], in1=bias_b_all[:, :, kv, :], op=ADD
+            )
+
+        def store(r, kv):
+            g, first = divmod(r * ROUND_TILES, GROUP_TILES)
+            nc.sync.dma_start(
+                out=out_groups[kv][g][:, first : first + ROUND_TILES, :],
+                in_=result[r][:, kv].rearrange("p s h c -> p s (h c)"),
+            )
+
+        done = set()
+
+        def once(step, *where):
+            if (step, where) not in done:
+                done.add((step, where))
+                step(*where)
+
+        once(transpose_x, 0)
+        once(regroup_x, 0)
+        once(quantise_x, 0)
+        once(transpose_wb, 0)
+        once(transpose_x, 1)
+        once(regroup_x, 1)
+        once(first_matmul, 0, 0)
+        once(first_matmul, 0, 1)
+        once(quantise_x, 1)
+        once(regroup_wb, 0)
+        once(square, 0, 0)
+        once(bias_and_gain, 0, 1)
+        once(square, 0, 1)
+        once(bias_and_gain, 0, 0)
+        once(quantise_wb, 0)
+        once(transpose_wb, 1)
+        once(transpose_x, 2)
+        once(add_squares, 0)
+        once(first_matmul, 1, 0)
+        once(first_matmul, 1, 1)
+        once(regroup_x, 2)
+        once(quantise_x, 2)
+        once(inverse_root, 0)
+        once(square, 1, 0)
+        once(bias_and_gain, 1, 1)
+        once(square, 1, 1)
+        once(bias_and_gain, 1, 0)
+        once(spread_rstd, 0)
+        once(regroup_wb, 1)
+        once(normalise_vector, 0)
+        once(quantise_latent, 0)
+        once(add_squares, 1)
+        X_AHEAD = 6
+        for n in range(-X_AHEAD, ROUNDS):
+            if live(n + 3):
+                once(square, n + 3, 0)
+                once(bias_and_gain, n + 3, 0)
             if live(n + 2):
-                quantise_x(n + 2)
-            if live(n - 1):
-                quantise_latent(n - 1)
+                once(inverse_root, n + 2)
+            if live(n + 5):
+                once(regroup_x, n + 5)
+            if live(n + 3):
+                once(square, n + 3, 1)
+                once(bias_and_gain, n + 3, 1)
+            if live(n + 1):
+                once(normalise_gpsimd, n + 1)
+                once(normalise_vector, n + 1)
+            if live(n):
+                once(second_matmul, n, 0)
+                once(add_second_bias, n, 0, 0)
+                once(add_second_bias, n, 0, 1)
+                once(second_matmul, n, 1)
+                once(add_second_bias, n, 1, 0)
+                once(store, n, 0)
+                once(add_second_bias, n, 1, 1)
+                once(store, n, 1)
+            if live(n + 4):
+                once(first_matmul, n + 4, 0)
+            if live(n + 2):
+                once(spread_rstd, n + 2)
+                once(fetch_factor, n + 2)
+            if live(n + 6):
+                once(transpose_x, n + 6)
+            if 0 <= n + 5 < HEADS:
+                once(transpose_wb, n + 5)
+                once(regroup_wb, n + 5)
+                once(quantise_wb, n + 5)
+            if n == -1:
+                once(spread_bias_b)
+            if live(n + 3):
+                once(add_squares, n + 3)
+            if live(n + 5):
+                once(quantise_x, n + 5)
+            if live(n + 1):
+                once(quantise_latent, n + 1)
+            if live(n + 4):
+                once(first_matmul, n + 4, 1)

@@ -388,46 +388,47 @@ def tile_mla_pa_t_kernel(
         once(add_squares, 1)
         X_AHEAD = 6
         for n in range(-X_AHEAD, ROUNDS):
+            if live(n + 5):
+                once(regroup_x, n + 5)
             if live(n + 3):
                 once(square, n + 3, 0)
                 once(bias_and_gain, n + 3, 0)
             if live(n + 2):
                 once(inverse_root, n + 2)
-            if live(n + 5):
-                once(regroup_x, n + 5)
             if live(n + 3):
                 once(square, n + 3, 1)
                 once(bias_and_gain, n + 3, 1)
-            if live(n + 1):
-                once(normalise_gpsimd, n + 1)
-                once(normalise_vector, n + 1)
             if live(n):
                 once(second_matmul, n, 0)
                 once(add_second_bias, n, 0, 0)
                 once(add_second_bias, n, 0, 1)
                 once(second_matmul, n, 1)
-                once(add_second_bias, n, 1, 0)
-                once(store, n, 0)
-                once(add_second_bias, n, 1, 1)
-                once(store, n, 1)
+            if live(n + 5):
+                once(quantise_x, n + 5)
+            if live(n + 1):
+                once(quantise_latent, n + 1)
             if live(n + 4):
                 once(first_matmul, n + 4, 0)
             if live(n + 2):
                 once(spread_rstd, n + 2)
                 once(fetch_factor, n + 2)
+                once(normalise_gpsimd, n + 2)
             if live(n + 6):
                 once(transpose_x, n + 6)
             if 0 <= n + 5 < HEADS:
                 once(transpose_wb, n + 5)
-                once(regroup_wb, n + 5)
+                regroup_wb(n + 5)
                 once(quantise_wb, n + 5)
             if n == -1:
                 once(spread_bias_b)
             if live(n + 3):
                 once(add_squares, n + 3)
-            if live(n + 5):
-                once(quantise_x, n + 5)
-            if live(n + 1):
-                once(quantise_latent, n + 1)
+            if live(n):
+                once(add_second_bias, n, 1, 0)
+                once(store, n, 0)
+                once(add_second_bias, n, 1, 1)
+                once(store, n, 1)
+            if live(n + 2):
+                once(normalise_vector, n + 2)
             if live(n + 4):
                 once(first_matmul, n + 4, 1)

@@ -149,7 +149,8 @@ def tile_mla_pa_t_kernel(
 
         def regroup_wb(h):
             wb_grouped[h] = work.tile([P, KV, HEAD, PACK], BF16, align_bytes=64, name="wb_grouped")
-            nc.scalar.copy(out=wb_grouped[h][:].bitcast(F32), in_=pair_words(wb_banks[h]))
+            copy = nc.vector.tensor_copy if h % 3 == 0 else nc.scalar.copy
+            copy(out=wb_grouped[h][:].bitcast(F32), in_=pair_words(wb_banks[h]))
 
         def quantise_wb(h):
             for s in range(KV):
@@ -161,17 +162,27 @@ def tile_mla_pa_t_kernel(
 
         bias_b_all = keep.tile([P, HEADS, KV, HEAD], BF16)
 
+        spread_banks = {}
+
         def spread_bias_b():
+            for b in range(KV):
+                spread_banks[b] = psum_o.tile([P, K], F32, tag="o", name="spread_bank")
+                nc.tensor.matmul(
+                    out=spread_banks[b][:],
+                    lhsT=ones_bf[:],
+                    rhs=bias_b_row[:, block(b, K)],
+                    start=True,
+                    stop=True,
+                )
+
+        def keep_bias_b():
             flat = bias_b_all[:].rearrange("p h s c -> p (h s c)")
             for b in range(KV):
-                bank = psum_o.tile([P, K], F32, tag="o", name="spread_bank")
-                nc.tensor.matmul(
-                    out=bank[:], lhsT=ones_bf[:], rhs=bias_b_row[:, block(b, K)], start=True, stop=True
-                )
-                nc.scalar.copy(out=flat[:, block(b, K)], in_=bank[:])
+                nc.scalar.copy(out=flat[:, block(b, K)], in_=spread_banks[b][:])
 
         x_bank, x_grouped, x_codes, x_scales = {}, {}, {}, {}
-        c_bank, y, squares, q_bank, rstd, factor_bank, factor = {}, {}, {}, {}, {}, {}, {}
+        c_bank, y, squares, q_bank, sum_sq, rstd = {}, {}, {}, {}, {}, {}
+        factor_bank, factor = {}, {}
         l_grouped, l_codes, l_scales = {}, {}, {}
         o_bank, result = {}, {}
 
@@ -260,13 +271,15 @@ def tile_mla_pa_t_kernel(
                         stop=(j == PACK - 1),
                     )
 
+        def sum_features(r):
+            sum_sq[r] = work.tile([P, ROUND_TILES], F32, name="sum_sq")
+            nc.vector.tensor_reduce(out=sum_sq[r][:], in_=q_bank[r][:], op=ADD, axis=AXIS_X)
+
         def inverse_root(r):
-            sum_sq = work.tile([P, ROUND_TILES], F32, name="sum_sq")
-            nc.vector.tensor_reduce(out=sum_sq[:], in_=q_bank[r][:], op=ADD, axis=AXIS_X)
             rstd[r] = work.tile([P, ROUND_TILES], F32, name="rstd")
             nc.scalar.activation(
                 out=rstd[r][:],
-                in_=sum_sq[:],
+                in_=sum_sq[r][:],
                 func=ACT.Abs_reciprocal_sqrt,
                 scale=1.0 / K,
                 bias=eps[:],
@@ -355,37 +368,116 @@ def tile_mla_pa_t_kernel(
                 step(*where)
 
         once(transpose_x, 0)
-        once(regroup_x, 0)
-        once(quantise_x, 0)
-        once(transpose_wb, 0)
         once(transpose_x, 1)
+        once(transpose_wb, 0)
+        once(regroup_x, 0)
         once(regroup_x, 1)
+        once(quantise_x, 0)
+        once(regroup_wb, 0)
+        once(transpose_wb, 1)
+        once(transpose_wb, 2)
+        once(quantise_x, 1)
+        once(regroup_wb, 1)
+        once(quantise_wb, 0)
         once(first_matmul, 0, 0)
         once(first_matmul, 0, 1)
-        once(quantise_x, 1)
-        once(regroup_wb, 0)
+        once(transpose_wb, 3)
+        once(transpose_x, 2)
         once(square, 0, 0)
         once(bias_and_gain, 0, 1)
         once(square, 0, 1)
         once(bias_and_gain, 0, 0)
-        once(quantise_wb, 0)
-        once(transpose_wb, 1)
-        once(transpose_x, 2)
+        once(quantise_wb, 1)
         once(add_squares, 0)
-        once(first_matmul, 1, 0)
         once(first_matmul, 1, 1)
+        once(first_matmul, 1, 0)
+        once(regroup_wb, 2)
+        once(regroup_wb, 3)
         once(regroup_x, 2)
-        once(quantise_x, 2)
+        once(spread_bias_b)
+        once(sum_features, 0)
         once(inverse_root, 0)
-        once(square, 1, 0)
-        once(bias_and_gain, 1, 1)
+        once(quantise_x, 2)
+        once(quantise_wb, 2)
         once(square, 1, 1)
         once(bias_and_gain, 1, 0)
+        once(square, 1, 0)
+        once(bias_and_gain, 1, 1)
         once(spread_rstd, 0)
-        once(regroup_wb, 1)
-        once(normalise_vector, 0)
-        once(quantise_latent, 0)
+        once(transpose_x, 3)
         once(add_squares, 1)
+        once(keep_bias_b)
+        once(quantise_wb, 3)
+        once(sum_features, 1)
+        once(normalise_vector, 0)
+        once(first_matmul, 2, 0)
+        once(first_matmul, 2, 1)
+        once(regroup_x, 3)
+        once(transpose_x, 4)
+        once(quantise_latent, 0)
+        once(inverse_root, 1)
+        once(quantise_x, 3)
+        once(square, 2, 0)
+        once(square, 2, 1)
+        once(second_matmul, 0, 0)
+        once(spread_rstd, 1)
+        once(add_second_bias, 0, 0, 0)
+        once(add_second_bias, 0, 0, 1)
+        once(add_squares, 2)
+        once(sum_features, 2)
+        once(normalise_vector, 1)
+        once(bias_and_gain, 2, 0)
+        once(bias_and_gain, 2, 1)
+        once(first_matmul, 3, 0)
+        once(first_matmul, 3, 1)
+        once(regroup_x, 4)
+        once(second_matmul, 0, 1)
+        once(transpose_x, 5)
+        once(quantise_latent, 1)
+        once(quantise_x, 4)
+        once(square, 3, 0)
+        once(square, 3, 1)
+        once(inverse_root, 2)
+        once(add_second_bias, 0, 1, 0)
+        once(store, 0, 0)
+        once(add_second_bias, 0, 1, 1)
+        once(store, 0, 1)
+        once(spread_rstd, 2)
+        once(bias_and_gain, 3, 0)
+        once(bias_and_gain, 3, 1)
+        once(fetch_factor, 2)
+        once(normalise_gpsimd, 2)
+        once(add_squares, 3)
+        once(second_matmul, 1, 0)
+        once(first_matmul, 4, 0)
+        once(first_matmul, 4, 1)
+        once(add_second_bias, 1, 0, 0)
+        once(add_second_bias, 1, 0, 1)
+        once(regroup_x, 5)
+        once(sum_features, 3)
+        once(normalise_vector, 2)
+        once(second_matmul, 1, 1)
+        once(transpose_x, 6)
+        once(square, 4, 0)
+        once(bias_and_gain, 4, 0)
+        once(inverse_root, 3)
+        once(square, 4, 1)
+        once(add_second_bias, 1, 1, 0)
+        once(store, 1, 0)
+        once(add_second_bias, 1, 1, 1)
+        once(store, 1, 1)
+        once(bias_and_gain, 4, 1)
+        once(regroup_x, 6)
+        once(quantise_x, 5)
+        once(quantise_latent, 2)
+        once(spread_rstd, 3)
+        once(fetch_factor, 3)
+        once(normalise_gpsimd, 3)
+        once(add_squares, 4)
+        once(transpose_x, 7)
+        once(first_matmul, 5, 0)
+        once(regroup_x, 7)
+        once(first_matmul, 5, 1)
         X_AHEAD = 6
         for n in range(-X_AHEAD, ROUNDS):
             if live(n + 5):
@@ -394,6 +486,7 @@ def tile_mla_pa_t_kernel(
                 once(square, n + 3, 0)
                 once(bias_and_gain, n + 3, 0)
             if live(n + 2):
+                once(sum_features, n + 2)
                 once(inverse_root, n + 2)
             if live(n + 3):
                 once(square, n + 3, 1)
@@ -417,10 +510,11 @@ def tile_mla_pa_t_kernel(
                 once(transpose_x, n + 6)
             if 0 <= n + 5 < HEADS:
                 once(transpose_wb, n + 5)
-                regroup_wb(n + 5)
+                once(regroup_wb, n + 5)
                 once(quantise_wb, n + 5)
             if n == -1:
                 once(spread_bias_b)
+                once(keep_bias_b)
             if live(n + 3):
                 once(add_squares, n + 3)
             if live(n):

@@ -73,23 +73,42 @@ def tile_mla_pa_t_kernel(
         psum_o = stack.enter_context(tc.psum_pool(name="psum_o", bufs=4))
         stack.enter_context(tc.manual_schedule())
 
-        bias_b_row = keep.tile([P, HEADS * KV * HEAD], BF16)
-        nc.vector.memset(bias_b_row[:], 0.0)
         bias_a_bf = keep.tile([P, PACK], BF16)
         gain_bf = keep.tile([P, PACK], BF16)
+        bias_b_all = keep.tile([P, HEADS, KV, HEAD], BF16)
         wa_sb = keep.tile([P, PACK, K], BF16)
         wb_sb = keep.tile([P, HEADS, KV, K], BF16)
         x_sb = keep.tile([P, GROUPS, GROUP_TILES * K], BF16)
-        nc.sync.dma_start(out=wa_sb[:], in_=wkv_a_w.rearrange("(p j) d -> p j d", j=PACK))
-        nc.sync.dma_start(out=x_sb[:, 0, :], in_=x_groups[0])
+
+        def load_x(g, half):
+            cols = block(half, ROUND_TILES * K)
+            nc.sync.dma_start(out=x_sb[:, g, cols], in_=x_groups[g][:, cols])
+
+        wa_rows = wkv_a_w.rearrange("(p j) d -> p j d", j=PACK)
+        for b in range(2):
+            nc.sync.dma_start(out=wa_sb[:, block(b, 2), :], in_=wa_rows[:, block(b, 2), :])
         nc.scalar.dma_start(out=bias_a_bf[:], in_=wkv_a_b.rearrange("(p j) -> p j", j=PACK))
         nc.scalar.dma_start(out=gain_bf[:], in_=kv_norm_w.rearrange("(p j) -> p j", j=PACK))
-        nc.scalar.dma_start(out=bias_b_row[0:1, :], in_=wkv_b_b.rearrange("(o n) -> o n", o=1))
         wb_heads = wkv_b_w.rearrange("(h s p) r -> h p s r", s=KV, p=P)
-        for h in range(HEADS):
+
+        def load_wb(h):
             nc.sync.dma_start(out=wb_sb[:, h], in_=wb_heads[h])
-        for g in range(1, GROUPS):
+
+        load_x(0, 0)
+        load_x(0, 1)
+        load_wb(0)
+        load_x(1, 0)
+        load_wb(1)
+        load_x(1, 1)
+        load_wb(2)
+        load_wb(3)
+        for g in range(2, GROUPS):
             nc.sync.dma_start(out=x_sb[:, g, :], in_=x_groups[g])
+            if g == 3:
+                nc.sync.dma_start(
+                    out=bias_b_all[:].rearrange("p h s c -> p (h s c)"),
+                    in_=wkv_b_b.partition_broadcast(P),
+                )
 
         ident = keep.tile([P, P], F32)
         make_identity(nc, ident[:])
@@ -99,8 +118,6 @@ def tile_mla_pa_t_kernel(
         one = keep.tile([P, 1], F32)
         nc.vector.memset(one[:], 1.0)
         nc.scalar.activation(out=one[:], in_=one[:], func=ACT.Abs_reciprocal_sqrt)
-        ones_bf = keep.tile([P, P], BF16)
-        nc.vector.memset(ones_bf[:], 1.0)
 
         bias_a = keep.tile([P, PACK], F32)
         gain = keep.tile([P, PACK], F32)
@@ -159,26 +176,6 @@ def tile_mla_pa_t_kernel(
                     scales=wb_scales[:, s, h, :],
                     in_=wb_grouped[h][:, s].rearrange("p m j -> p (m j)"),
                 )
-
-        bias_b_all = keep.tile([P, HEADS, KV, HEAD], BF16)
-
-        spread_banks = {}
-
-        def spread_bias_b():
-            for b in range(KV):
-                spread_banks[b] = psum_o.tile([P, K], F32, tag="o", name="spread_bank")
-                nc.tensor.matmul(
-                    out=spread_banks[b][:],
-                    lhsT=ones_bf[:],
-                    rhs=bias_b_row[:, block(b, K)],
-                    start=True,
-                    stop=True,
-                )
-
-        def keep_bias_b():
-            flat = bias_b_all[:].rearrange("p h s c -> p (h s c)")
-            for b in range(KV):
-                nc.scalar.copy(out=flat[:, block(b, K)], in_=spread_banks[b][:])
 
         x_bank, x_grouped, x_codes, x_scales = {}, {}, {}, {}
         c_bank, y, squares, q_bank, sum_sq, rstd = {}, {}, {}, {}, {}, {}
@@ -353,11 +350,11 @@ def tile_mla_pa_t_kernel(
                 out=result[r][:, kv, s], in0=o_bank[r, s, kv][:], in1=bias_b_all[:, :, kv, :], op=ADD
             )
 
-        def store(r, kv):
-            g, first = divmod(r * ROUND_TILES, GROUP_TILES)
+        def store(r, kv, first=0, count=ROUND_TILES):
+            g, tile = divmod(r * ROUND_TILES + first, GROUP_TILES)
             nc.sync.dma_start(
-                out=out_groups[kv][g][:, first : first + ROUND_TILES, :],
-                in_=result[r][:, kv].rearrange("p s h c -> p s (h c)"),
+                out=out_groups[kv][g][:, tile : tile + count, :],
+                in_=result[r][:, kv, first : first + count].rearrange("p s h c -> p s (h c)"),
             )
 
         done = set()
@@ -369,36 +366,31 @@ def tile_mla_pa_t_kernel(
 
         once(transpose_x, 0)
         once(transpose_x, 1)
-        once(transpose_wb, 0)
         once(regroup_x, 0)
         once(regroup_x, 1)
         once(quantise_x, 0)
-        once(regroup_wb, 0)
-        once(transpose_wb, 1)
-        once(transpose_wb, 2)
-        once(quantise_x, 1)
-        once(regroup_wb, 1)
-        once(quantise_wb, 0)
+        once(transpose_wb, 0)
         once(first_matmul, 0, 0)
         once(first_matmul, 0, 1)
-        once(transpose_wb, 3)
+        once(regroup_wb, 0)
+        once(quantise_x, 1)
         once(transpose_x, 2)
+        once(transpose_wb, 1)
         once(square, 0, 0)
         once(bias_and_gain, 0, 1)
         once(square, 0, 1)
         once(bias_and_gain, 0, 0)
-        once(quantise_wb, 1)
+        once(quantise_wb, 0)
         once(add_squares, 0)
         once(first_matmul, 1, 1)
         once(first_matmul, 1, 0)
-        once(regroup_wb, 2)
-        once(regroup_wb, 3)
         once(regroup_x, 2)
-        once(spread_bias_b)
+        once(regroup_wb, 1)
         once(sum_features, 0)
         once(inverse_root, 0)
         once(quantise_x, 2)
-        once(quantise_wb, 2)
+        once(transpose_wb, 2)
+        once(transpose_wb, 3)
         once(square, 1, 1)
         once(bias_and_gain, 1, 0)
         once(square, 1, 0)
@@ -406,16 +398,19 @@ def tile_mla_pa_t_kernel(
         once(spread_rstd, 0)
         once(transpose_x, 3)
         once(add_squares, 1)
-        once(keep_bias_b)
-        once(quantise_wb, 3)
+        once(quantise_wb, 1)
+        once(regroup_wb, 2)
+        once(regroup_wb, 3)
         once(sum_features, 1)
         once(normalise_vector, 0)
         once(first_matmul, 2, 0)
         once(first_matmul, 2, 1)
         once(regroup_x, 3)
-        once(transpose_x, 4)
+        once(quantise_wb, 2)
         once(quantise_latent, 0)
+        once(transpose_x, 4)
         once(inverse_root, 1)
+        once(quantise_wb, 3)
         once(quantise_x, 3)
         once(square, 2, 0)
         once(square, 2, 1)
@@ -495,6 +490,9 @@ def tile_mla_pa_t_kernel(
                 once(second_matmul, n, 0)
                 once(add_second_bias, n, 0, 0)
                 once(add_second_bias, n, 0, 1)
+                if n >= ROUNDS - 2:
+                    for kv in range(KV):
+                        store(n, kv, 0, 1)
                 once(second_matmul, n, 1)
             if live(n + 5):
                 once(quantise_x, n + 5)
@@ -512,16 +510,19 @@ def tile_mla_pa_t_kernel(
                 once(transpose_wb, n + 5)
                 once(regroup_wb, n + 5)
                 once(quantise_wb, n + 5)
-            if n == -1:
-                once(spread_bias_b)
-                once(keep_bias_b)
             if live(n + 3):
                 once(add_squares, n + 3)
             if live(n):
                 once(add_second_bias, n, 1, 0)
-                once(store, n, 0)
+                if n >= ROUNDS - 2:
+                    store(n, 0, 1, 1)
+                else:
+                    once(store, n, 0)
                 once(add_second_bias, n, 1, 1)
-                once(store, n, 1)
+                if n >= ROUNDS - 2:
+                    store(n, 1, 1, 1)
+                else:
+                    once(store, n, 1)
             if live(n + 2):
                 once(normalise_vector, n + 2)
             if live(n + 4):

@@ -67,7 +67,7 @@ def tile_mla_pa_t_kernel(
         keep = stack.enter_context(tc.tile_pool(name="keep", bufs=1))
         work = stack.enter_context(tc.tile_pool(name="work", bufs=4))
         single = stack.enter_context(tc.tile_pool(name="single", bufs=1))
-        stage = stack.enter_context(tc.tile_pool(name="stage", bufs=4))
+        stage = stack.enter_context(tc.tile_pool(name="stage", bufs=12))
         psum_c = stack.enter_context(tc.psum_pool(name="psum_c", bufs=1))
         psum_s = stack.enter_context(tc.psum_pool(name="psum_s", bufs=1))
         psum_o = stack.enter_context(tc.psum_pool(name="psum_o", bufs=4))
@@ -87,8 +87,6 @@ def tile_mla_pa_t_kernel(
         wa_rows = wkv_a_w.rearrange("(p j) d -> p j d", j=PACK)
         for b in range(2):
             nc.sync.dma_start(out=wa_sb[:, block(b, 2), :], in_=wa_rows[:, block(b, 2), :])
-        nc.scalar.dma_start(out=bias_a_bf[:], in_=wkv_a_b.rearrange("(p j) -> p j", j=PACK))
-        nc.scalar.dma_start(out=gain_bf[:], in_=kv_norm_w.rearrange("(p j) -> p j", j=PACK))
         wb_heads = wkv_b_w.rearrange("(h s p) r -> h p s r", s=KV, p=P)
 
         def load_wb(h):
@@ -96,6 +94,8 @@ def tile_mla_pa_t_kernel(
 
         load_x(0, 0)
         load_x(0, 1)
+        nc.sync.dma_start(out=bias_a_bf[:], in_=wkv_a_b.rearrange("(p j) -> p j", j=PACK))
+        nc.sync.dma_start(out=gain_bf[:], in_=kv_norm_w.rearrange("(p j) -> p j", j=PACK))
         load_wb(0)
         load_x(1, 0)
         load_wb(1)
@@ -110,6 +110,8 @@ def tile_mla_pa_t_kernel(
                     in_=wkv_b_b.partition_broadcast(P),
                 )
 
+        zeros = keep.tile([P, K], BF16)
+        nc.vector.memset(zeros[:], 0.0)
         ident = keep.tile([P, P], F32)
         make_identity(nc, ident[:])
         eps = keep.tile([P, 1], F32)
@@ -119,12 +121,12 @@ def tile_mla_pa_t_kernel(
         nc.vector.memset(one[:], 1.0)
         nc.scalar.activation(out=one[:], in_=one[:], func=ACT.Abs_reciprocal_sqrt)
 
-        bias_a = keep.tile([P, PACK], F32)
-        gain = keep.tile([P, PACK], F32)
-        gained_bias = keep.tile([P, PACK], F32)
-        nc.vector.tensor_copy(out=bias_a[:], in_=bias_a_bf[:])
-        nc.vector.tensor_copy(out=gain[:], in_=gain_bf[:])
-        nc.vector.tensor_tensor(out=gained_bias[:], in0=bias_a[:], in1=gain[:], op=MULT)
+        def keep_warm(count):
+            bank = psum_s.tile([P, K], F32, tag="q", name="warm_bank")
+            for i in range(count):
+                nc.tensor.matmul(out=bank[:], lhsT=zeros[:, 0:P], rhs=zeros[:], start=True, stop=True)
+
+        keep_warm(4)
 
         def transpose_words(bank, rows):
             for s in range(len(rows)):
@@ -153,6 +155,13 @@ def tile_mla_pa_t_kernel(
             scales=wa_scales[:],
             in_=wa_grouped[:].rearrange("p m j -> p (m j)"),
         )
+
+        bias_a = keep.tile([P, PACK], F32)
+        gain = keep.tile([P, PACK], F32)
+        gained_bias = keep.tile([P, PACK], F32)
+        nc.vector.tensor_copy(out=bias_a[:], in_=bias_a_bf[:])
+        nc.vector.tensor_copy(out=gain[:], in_=gain_bf[:])
+        nc.vector.tensor_tensor(out=gained_bias[:], in0=bias_a[:], in1=gain[:], op=MULT)
 
         wb_codes = keep.tile([P, KV, HEADS, HEAD], U32, align_bytes=64)
         wb_scales = keep.tile([P, KV, HEADS, HEAD], U8, align_bytes=64)
@@ -370,6 +379,7 @@ def tile_mla_pa_t_kernel(
         once(regroup_x, 1)
         once(quantise_x, 0)
         once(transpose_wb, 0)
+        keep_warm(2)
         once(first_matmul, 0, 0)
         once(first_matmul, 0, 1)
         once(regroup_wb, 0)
@@ -396,33 +406,33 @@ def tile_mla_pa_t_kernel(
         once(square, 1, 0)
         once(bias_and_gain, 1, 1)
         once(spread_rstd, 0)
-        once(transpose_x, 3)
+        once(first_matmul, 2, 0)
+        once(first_matmul, 2, 1)
         once(add_squares, 1)
+        once(transpose_x, 3)
         once(quantise_wb, 1)
         once(regroup_wb, 2)
         once(regroup_wb, 3)
-        once(sum_features, 1)
         once(normalise_vector, 0)
-        once(first_matmul, 2, 0)
-        once(first_matmul, 2, 1)
+        once(square, 2, 0)
+        once(square, 2, 1)
+        once(sum_features, 1)
         once(regroup_x, 3)
         once(quantise_wb, 2)
         once(quantise_latent, 0)
-        once(transpose_x, 4)
         once(inverse_root, 1)
-        once(quantise_wb, 3)
         once(quantise_x, 3)
-        once(square, 2, 0)
-        once(square, 2, 1)
+        once(quantise_wb, 3)
+        once(bias_and_gain, 2, 0)
+        once(bias_and_gain, 2, 1)
+        once(add_squares, 2)
+        once(transpose_x, 4)
         once(second_matmul, 0, 0)
         once(spread_rstd, 1)
         once(add_second_bias, 0, 0, 0)
         once(add_second_bias, 0, 0, 1)
-        once(add_squares, 2)
         once(sum_features, 2)
         once(normalise_vector, 1)
-        once(bias_and_gain, 2, 0)
-        once(bias_and_gain, 2, 1)
         once(first_matmul, 3, 0)
         once(first_matmul, 3, 1)
         once(regroup_x, 4)

@@ -138,8 +138,8 @@ def tile_mla_pa_t_kernel(
             return bank[:].rearrange("p s u m -> p s m u")
 
         wa_grouped = keep.tile([P, K, PACK], BF16, align_bytes=64)
-        wa_codes = keep.tile([P, K], U32, align_bytes=64)
-        wa_scales = keep.tile([P, K], U8, align_bytes=64)
+        wa_codes = keep.tile([P, K], U32, align_bytes=256)
+        wa_scales = keep.tile([P, K], U8, align_bytes=256)
         for b in range(2):
             wa_bank = psum_o.tile([P, 2, WORDS, P], F32, tag="o")
             transpose_words(wa_bank, [wa_sb[:, 2 * b + s, :] for s in range(2)])
@@ -163,8 +163,8 @@ def tile_mla_pa_t_kernel(
         nc.vector.tensor_copy(out=gain[:], in_=gain_bf[:])
         nc.vector.tensor_tensor(out=gained_bias[:], in0=bias_a[:], in1=gain[:], op=MULT)
 
-        wb_codes = keep.tile([P, KV, HEADS, HEAD], U32, align_bytes=64)
-        wb_scales = keep.tile([P, KV, HEADS, HEAD], U8, align_bytes=64)
+        wb_codes = keep.tile([P, KV, HEADS, HEAD], U32, align_bytes=256)
+        wb_scales = keep.tile([P, KV, HEADS, HEAD], U8, align_bytes=256)
         wb_banks = {}
 
         def transpose_wb(h):
@@ -207,8 +207,8 @@ def tile_mla_pa_t_kernel(
             copy(out=x_grouped[r][:].bitcast(F32), in_=pair_words(x_bank[r]))
 
         def quantise_x(r):
-            x_codes[r] = work.tile([P, COLS], U32, align_bytes=64, name="x_codes")
-            x_scales[r] = work.tile([P, COLS], U8, align_bytes=64, name="x_scales")
+            x_codes[r] = work.tile([P, COLS], U32, align_bytes=256, name="x_codes")
+            x_scales[r] = work.tile([P, COLS], U8, align_bytes=256, name="x_scales")
             nc.vector.quantize_mx(
                 out=x_codes[r][:].bitcast(FP8X4),
                 scales=x_scales[r][:],
@@ -331,8 +331,8 @@ def tile_mla_pa_t_kernel(
                 normalise(r, cols, nc.vector, factor_bank[r][:].rearrange("p s m -> p (s m)")[:, cols])
 
         def quantise_latent(r):
-            l_codes[r] = work.tile([P, COLS], U32, align_bytes=64, name="l_codes")
-            l_scales[r] = work.tile([P, COLS], U8, align_bytes=64, name="l_scales")
+            l_codes[r] = work.tile([P, COLS], U32, align_bytes=256, name="l_codes")
+            l_scales[r] = work.tile([P, COLS], U8, align_bytes=256, name="l_scales")
             nc.vector.quantize_mx(
                 out=l_codes[r][:].bitcast(FP8X4),
                 scales=l_scales[r][:],

@@ -50,7 +50,7 @@ def gain_on_vector(r):
 
 
 def gpsimd_cols(r):
-    return 0 if r < 2 else 192
+    return 0 if r < 2 else 208
 
 
 def tile_mla_pa_t_kernel(
@@ -355,16 +355,25 @@ def tile_mla_pa_t_kernel(
         def add_second_bias(r, s, kv):
             if s == 0 and kv == 0:
                 result[r] = stage.tile([P, KV, ROUND_TILES, HEADS, HEAD], F32, name="result")
-            nc.vector.tensor_tensor(
-                out=result[r][:, kv, s], in0=o_bank[r, s, kv][:], in1=bias_b_all[:, :, kv, :], op=ADD
-            )
+            for heads in ((slice(0, 2), slice(2, 4)) if (r, s, kv) == (ROUNDS - 1, 1, 1) else (slice(0, 4),)):
+                nc.vector.tensor_tensor(
+                    out=result[r][:, kv, s, heads],
+                    in0=o_bank[r, s, kv][:, heads],
+                    in1=bias_b_all[:, heads, kv, :],
+                    op=ADD,
+                )
 
         def store(r, kv, first=0, count=ROUND_TILES):
             g, tile = divmod(r * ROUND_TILES + first, GROUP_TILES)
-            nc.sync.dma_start(
-                out=out_groups[kv][g][:, tile : tile + count, :],
-                in_=result[r][:, kv, first : first + count].rearrange("p s h c -> p s (h c)"),
-            )
+            for heads in ((slice(0, 2), slice(2, 4)) if (r, first, kv) == (ROUNDS - 1, 1, 1) else (slice(0, 4),)):
+                nc.sync.dma_start(
+                    out=out_groups[kv][g][
+                        :, tile : tile + count, heads.start * HEAD : heads.stop * HEAD
+                    ],
+                    in_=result[r][:, kv, first : first + count, heads].rearrange(
+                        "p s h c -> p s (h c)"
+                    ),
+                )
 
         done = set()
 

@@ -22,6 +22,7 @@ HEADS = 4
 HEAD = 128
 KV = 2
 EPS = 1e-6
+RUN = 4
 
 GROUP_TILES = 4
 GROUPS = TOKENS // (P * GROUP_TILES)
@@ -313,9 +314,11 @@ def tile_mla_pa_t_kernel(
             if r not in l_grouped:
                 l_grouped[r] = single.tile([P, COLS, PACK], BF16, align_bytes=64, name="l_grouped")
             engine.tensor_tensor(
-                out=l_grouped[r][:, cols, :],
-                in0=y[r][:, :, cols].rearrange("p j m -> p m j"),
-                in1=factors.unsqueeze(2).to_broadcast([P, cols.stop - cols.start, PACK]),
+                out=l_grouped[r][:, cols, :].rearrange("p (c i) j -> p c j i", i=RUN),
+                in0=y[r][:, :, cols].rearrange("p j (c i) -> p c j i", i=RUN),
+                in1=factors.rearrange("p (c i) -> p c i", i=RUN)
+                .unsqueeze(2)
+                .to_broadcast([P, (cols.stop - cols.start) // RUN, PACK, RUN]),
                 op=MULT,
             )
 

@@ -51,7 +51,7 @@ def gain_on_vector(r):
 
 
 def gpsimd_cols(r):
-    return 0 if r < 2 else 208
+    return 0 if r < 2 else COLS
 
 
 def tile_mla_pa_t_kernel(

@@ -29,7 +29,7 @@ GROUPS = TOKENS // (P * GROUP_TILES)
 ROUND_TILES = 2
 ROUNDS = TOKENS // (P * ROUND_TILES)
 COLS = ROUND_TILES * P
-G_COLS = 192
+VECTOR_ROUNDS = 2
 
 FLOPS = 2 * TOKENS * K * K + 2 * TOKENS * K * (HEADS * KV * HEAD)
 
@@ -40,18 +40,6 @@ def block(i, width):
 
 def live(r):
     return 0 <= r < ROUNDS
-
-
-def regroup_on_vector(r):
-    return False
-
-
-def gain_on_vector(r):
-    return r < 2
-
-
-def gpsimd_cols(r):
-    return 0 if r < 2 else COLS
 
 
 def tile_mla_pa_t_kernel(
@@ -67,7 +55,7 @@ def tile_mla_pa_t_kernel(
     with ExitStack() as stack:
         keep = stack.enter_context(tc.tile_pool(name="keep", bufs=1))
         work = stack.enter_context(tc.tile_pool(name="work", bufs=4))
-        single = stack.enter_context(tc.tile_pool(name="single", bufs=1))
+        latent = stack.enter_context(tc.tile_pool(name="latent", bufs=2))
         stage = stack.enter_context(tc.tile_pool(name="stage", bufs=12))
         psum_c = stack.enter_context(tc.psum_pool(name="psum_c", bufs=1))
         psum_s = stack.enter_context(tc.psum_pool(name="psum_s", bufs=1))
@@ -151,11 +139,12 @@ def tile_mla_pa_t_kernel(
                 .rearrange("p (s m) u -> p s m u", s=2),
                 in_=pair_words(wa_bank),
             )
-        nc.vector.quantize_mx(
-            out=wa_codes[:].bitcast(FP8X4),
-            scales=wa_scales[:],
-            in_=wa_grouped[:].rearrange("p m j -> p (m j)"),
-        )
+        for b in range(2):
+            nc.vector.quantize_mx(
+                out=wa_codes[:, block(b, 2 * P)].bitcast(FP8X4),
+                scales=wa_scales[:, block(b, 2 * P)],
+                in_=wa_grouped[:, block(b, 2 * P), :].rearrange("p m j -> p (m j)"),
+            )
 
         bias_a = keep.tile([P, PACK], F32)
         gain = keep.tile([P, PACK], F32)
@@ -188,7 +177,7 @@ def tile_mla_pa_t_kernel(
                 )
 
         x_bank, x_grouped, x_codes, x_scales = {}, {}, {}, {}
-        c_bank, y, squares, q_bank, sum_sq, rstd = {}, {}, {}, {}, {}, {}
+        c_bank, y, squares, q_bank, sum_sq = {}, {}, {}, {}, {}
         factor_bank, factor = {}, {}
         l_grouped, l_codes, l_scales = {}, {}, {}
         o_bank, result = {}, {}
@@ -204,8 +193,7 @@ def tile_mla_pa_t_kernel(
             x_grouped[r] = work.tile(
                 [P, ROUND_TILES, P, PACK], BF16, align_bytes=64, name="x_grouped"
             )
-            copy = nc.vector.tensor_copy if regroup_on_vector(r) else nc.scalar.copy
-            copy(out=x_grouped[r][:].bitcast(F32), in_=pair_words(x_bank[r]))
+            nc.scalar.copy(out=x_grouped[r][:].bitcast(F32), in_=pair_words(x_bank[r]))
 
         def quantise_x(r):
             x_codes[r] = work.tile([P, COLS], U32, align_bytes=256, name="x_codes")
@@ -247,7 +235,7 @@ def tile_mla_pa_t_kernel(
                 y[r] = work.tile([P, PACK, COLS], F32, name="y")
             for e in range(2):
                 j = 2 * half + e
-                if gain_on_vector(r):
+                if r < VECTOR_ROUNDS:
                     nc.vector.tensor_scalar(
                         out=y[r][:, j, :],
                         in0=c_bank[r, half][:, e, :],
@@ -282,56 +270,37 @@ def tile_mla_pa_t_kernel(
             sum_sq[r] = work.tile([P, ROUND_TILES], F32, name="sum_sq")
             nc.vector.tensor_reduce(out=sum_sq[r][:], in_=q_bank[r][:], op=ADD, axis=AXIS_X)
 
+        def spread_sums(r):
+            factor_bank[r] = psum_s.tile([P, ROUND_TILES, P], F32, tag="f", name="factor_bank")
+            for s in range(ROUND_TILES):
+                nc.tensor.transpose(
+                    factor_bank[r][:, s, :],
+                    sum_sq[r][:, s : s + 1].to_broadcast([P, P]),
+                    ident[:],
+                )
+
         def inverse_root(r):
-            rstd[r] = work.tile([P, ROUND_TILES], F32, name="rstd")
+            factor[r] = work.tile([P, COLS], F32, name="factor")
             nc.scalar.activation(
-                out=rstd[r][:],
-                in_=sum_sq[r][:],
+                out=factor[r][:],
+                in_=factor_bank[r][:].rearrange("p s m -> p (s m)"),
                 func=ACT.Abs_reciprocal_sqrt,
                 scale=1.0 / K,
                 bias=eps[:],
             )
 
-        def spread_rstd(r):
-            factor_bank[r] = psum_s.tile([P, ROUND_TILES, P], F32, tag="f", name="factor_bank")
-            for s in range(ROUND_TILES):
-                nc.tensor.transpose(
-                    factor_bank[r][:, s, :],
-                    rstd[r][:, s : s + 1].to_broadcast([P, P]),
-                    ident[:],
-                )
-
-        def fetch_factor(r):
-            g = gpsimd_cols(r)
-            if g == 0:
-                return
-            factor[r] = work.tile([P, COLS], F32, name="factor")
-            nc.scalar.copy(
-                out=factor[r][:, 0:g], in_=factor_bank[r][:].rearrange("p s m -> p (s m)")[:, 0:g]
-            )
-
-        def normalise(r, cols, engine, factors):
-            if r not in l_grouped:
-                l_grouped[r] = single.tile([P, COLS, PACK], BF16, align_bytes=64, name="l_grouped")
+        def normalise(r):
+            l_grouped[r] = latent.tile([P, COLS, PACK], BF16, align_bytes=64, name="l_grouped")
+            engine = nc.vector if r < VECTOR_ROUNDS else nc.gpsimd
             engine.tensor_tensor(
-                out=l_grouped[r][:, cols, :].rearrange("p (c i) j -> p c j i", i=RUN),
-                in0=y[r][:, :, cols].rearrange("p j (c i) -> p c j i", i=RUN),
-                in1=factors.rearrange("p (c i) -> p c i", i=RUN)
+                out=l_grouped[r][:].rearrange("p (c i) j -> p c j i", i=RUN),
+                in0=y[r][:].rearrange("p j (c i) -> p c j i", i=RUN),
+                in1=factor[r][:]
+                .rearrange("p (c i) -> p c i", i=RUN)
                 .unsqueeze(2)
-                .to_broadcast([P, (cols.stop - cols.start) // RUN, PACK, RUN]),
+                .to_broadcast([P, COLS // RUN, PACK, RUN]),
                 op=MULT,
             )
-
-        def normalise_gpsimd(r):
-            g = gpsimd_cols(r)
-            if g > 0:
-                normalise(r, slice(0, g), nc.gpsimd, factor[r][:, 0:g])
-
-        def normalise_vector(r):
-            g = gpsimd_cols(r)
-            if g < COLS:
-                cols = slice(g, COLS)
-                normalise(r, cols, nc.vector, factor_bank[r][:].rearrange("p s m -> p (s m)")[:, cols])
 
         def quantise_latent(r):
             l_codes[r] = work.tile([P, COLS], U32, align_bytes=256, name="l_codes")
@@ -378,174 +347,62 @@ def tile_mla_pa_t_kernel(
                     ),
                 )
 
-        done = set()
+        def prepare_wb(h):
+            transpose_wb(h)
+            regroup_wb(h)
 
-        def once(step, *where):
-            if (step, where) not in done:
-                done.add((step, where))
-                step(*where)
-
-        once(transpose_x, 0)
-        once(transpose_x, 1)
-        once(regroup_x, 0)
-        once(regroup_x, 1)
-        once(quantise_x, 0)
-        once(transpose_wb, 0)
-        keep_warm(2)
-        once(first_matmul, 0, 0)
-        once(first_matmul, 0, 1)
-        once(regroup_wb, 0)
-        once(quantise_x, 1)
-        once(transpose_x, 2)
-        once(transpose_wb, 1)
-        once(square, 0, 0)
-        once(bias_and_gain, 0, 1)
-        once(square, 0, 1)
-        once(bias_and_gain, 0, 0)
-        once(quantise_wb, 0)
-        once(add_squares, 0)
-        once(first_matmul, 1, 1)
-        once(first_matmul, 1, 0)
-        once(regroup_x, 2)
-        once(regroup_wb, 1)
-        once(sum_features, 0)
-        once(inverse_root, 0)
-        once(quantise_x, 2)
-        once(transpose_wb, 2)
-        once(transpose_wb, 3)
-        once(square, 1, 1)
-        once(bias_and_gain, 1, 0)
-        once(square, 1, 0)
-        once(bias_and_gain, 1, 1)
-        once(spread_rstd, 0)
-        once(first_matmul, 2, 0)
-        once(first_matmul, 2, 1)
-        once(add_squares, 1)
-        once(transpose_x, 3)
-        once(quantise_wb, 1)
-        once(regroup_wb, 2)
-        once(regroup_wb, 3)
-        once(normalise_vector, 0)
-        once(square, 2, 0)
-        once(square, 2, 1)
-        once(sum_features, 1)
-        once(regroup_x, 3)
-        once(quantise_wb, 2)
-        once(quantise_latent, 0)
-        once(inverse_root, 1)
-        once(quantise_x, 3)
-        once(quantise_wb, 3)
-        once(bias_and_gain, 2, 0)
-        once(bias_and_gain, 2, 1)
-        once(add_squares, 2)
-        once(transpose_x, 4)
-        once(second_matmul, 0, 0)
-        once(spread_rstd, 1)
-        once(add_second_bias, 0, 0, 0)
-        once(add_second_bias, 0, 0, 1)
-        once(sum_features, 2)
-        once(normalise_vector, 1)
-        once(first_matmul, 3, 0)
-        once(first_matmul, 3, 1)
-        once(regroup_x, 4)
-        once(second_matmul, 0, 1)
-        once(transpose_x, 5)
-        once(quantise_latent, 1)
-        once(quantise_x, 4)
-        once(square, 3, 0)
-        once(square, 3, 1)
-        once(inverse_root, 2)
-        once(add_second_bias, 0, 1, 0)
-        once(store, 0, 0)
-        once(add_second_bias, 0, 1, 1)
-        once(store, 0, 1)
-        once(spread_rstd, 2)
-        once(bias_and_gain, 3, 0)
-        once(bias_and_gain, 3, 1)
-        once(fetch_factor, 2)
-        once(normalise_gpsimd, 2)
-        once(add_squares, 3)
-        once(second_matmul, 1, 0)
-        once(first_matmul, 4, 0)
-        once(first_matmul, 4, 1)
-        once(add_second_bias, 1, 0, 0)
-        once(add_second_bias, 1, 0, 1)
-        once(regroup_x, 5)
-        once(sum_features, 3)
-        once(normalise_vector, 2)
-        once(second_matmul, 1, 1)
-        once(transpose_x, 6)
-        once(square, 4, 0)
-        once(bias_and_gain, 4, 0)
-        once(inverse_root, 3)
-        once(square, 4, 1)
-        once(add_second_bias, 1, 1, 0)
-        once(store, 1, 0)
-        once(add_second_bias, 1, 1, 1)
-        once(store, 1, 1)
-        once(bias_and_gain, 4, 1)
-        once(regroup_x, 6)
-        once(quantise_x, 5)
-        once(quantise_latent, 2)
-        once(spread_rstd, 3)
-        once(fetch_factor, 3)
-        once(normalise_gpsimd, 3)
-        once(add_squares, 4)
-        once(transpose_x, 7)
-        once(first_matmul, 5, 0)
-        once(regroup_x, 7)
-        once(first_matmul, 5, 1)
-        X_AHEAD = 6
-        for n in range(-X_AHEAD, ROUNDS):
-            if live(n + 5):
-                once(regroup_x, n + 5)
-            if live(n + 3):
-                once(square, n + 3, 0)
-                once(bias_and_gain, n + 3, 0)
+        for n in range(-5, ROUNDS + 1):
+            if live(n - 1):
+                second_matmul(n - 1, 1)
+                for kv in range(KV):
+                    add_second_bias(n - 1, 1, kv)
+                    if n - 1 >= ROUNDS - 2:
+                        store(n - 1, kv, 1, 1)
+                    else:
+                        store(n - 1, kv)
+            if n == -3:
+                quantise_wb(1)
+                prepare_wb(2)
             if live(n + 2):
-                once(sum_features, n + 2)
-                once(inverse_root, n + 2)
+                add_squares(n + 2)
+                sum_features(n + 2)
             if live(n + 3):
-                once(square, n + 3, 1)
-                once(bias_and_gain, n + 3, 1)
+                first_matmul(n + 3, 1)
+            if live(n + 4):
+                quantise_x(n + 4)
+            if live(n + 3):
+                bias_and_gain(n + 3, 0)
+                bias_and_gain(n + 3, 1)
             if live(n):
-                once(second_matmul, n, 0)
-                once(add_second_bias, n, 0, 0)
-                once(add_second_bias, n, 0, 1)
+                second_matmul(n, 0)
+                add_second_bias(n, 0, 0)
+            if n == -4:
+                prepare_wb(0)
+            if live(n + 1):
+                quantise_latent(n + 1)
+            if n == -3:
+                quantise_wb(2)
+                prepare_wb(3)
+            if live(n + 2):
+                spread_sums(n + 2)
+                inverse_root(n + 2)
+                normalise(n + 2)
+            if live(n + 5):
+                transpose_x(n + 5)
+            if live(n):
+                add_second_bias(n, 0, 1)
                 if n >= ROUNDS - 2:
                     for kv in range(KV):
                         store(n, kv, 0, 1)
-                once(second_matmul, n, 1)
-            if live(n + 5):
-                once(quantise_x, n + 5)
-            if live(n + 1):
-                once(quantise_latent, n + 1)
-            if live(n + 4):
-                once(first_matmul, n + 4, 0)
-            if live(n + 2):
-                once(spread_rstd, n + 2)
-                once(fetch_factor, n + 2)
-                once(normalise_gpsimd, n + 2)
-            if live(n + 6):
-                once(transpose_x, n + 6)
-            if 0 <= n + 5 < HEADS:
-                once(transpose_wb, n + 5)
-                once(regroup_wb, n + 5)
-                once(quantise_wb, n + 5)
+            if n == -4:
+                quantise_wb(0)
+                prepare_wb(1)
             if live(n + 3):
-                once(add_squares, n + 3)
-            if live(n):
-                once(add_second_bias, n, 1, 0)
-                if n >= ROUNDS - 2:
-                    store(n, 0, 1, 1)
-                else:
-                    once(store, n, 0)
-                once(add_second_bias, n, 1, 1)
-                if n >= ROUNDS - 2:
-                    store(n, 1, 1, 1)
-                else:
-                    once(store, n, 1)
-            if live(n + 2):
-                once(normalise_vector, n + 2)
+                square(n + 3, 1)
+            if live(n + 5):
+                regroup_x(n + 5)
             if live(n + 4):
-                once(first_matmul, n + 4, 1)
+                first_matmul(n + 4, 0)
+                square(n + 4, 0)
+            if n == -3:
+                quantise_wb(3)

@@ -351,7 +351,7 @@ def tile_mla_pa_t_kernel(
             transpose_wb(h)
             regroup_wb(h)
 
-        for n in range(-5, ROUNDS + 1):
+        for n in range(-6, ROUNDS + 1):
             if live(n - 1):
                 second_matmul(n - 1, 1)
                 for kv in range(KV):
@@ -368,8 +368,6 @@ def tile_mla_pa_t_kernel(
                 sum_features(n + 2)
             if live(n + 3):
                 first_matmul(n + 3, 1)
-            if live(n + 4):
-                quantise_x(n + 4)
             if live(n + 3):
                 bias_and_gain(n + 3, 0)
                 bias_and_gain(n + 3, 1)
@@ -380,6 +378,8 @@ def tile_mla_pa_t_kernel(
                 prepare_wb(0)
             if live(n + 1):
                 quantise_latent(n + 1)
+            if live(n + 5):
+                quantise_x(n + 5)
             if n == -3:
                 quantise_wb(2)
                 prepare_wb(3)
@@ -387,8 +387,8 @@ def tile_mla_pa_t_kernel(
                 spread_sums(n + 2)
                 inverse_root(n + 2)
                 normalise(n + 2)
-            if live(n + 5):
-                transpose_x(n + 5)
+            if live(n + 6):
+                transpose_x(n + 6)
             if live(n):
                 add_second_bias(n, 0, 1)
                 if n >= ROUNDS - 2:
@@ -399,8 +399,8 @@ def tile_mla_pa_t_kernel(
                 prepare_wb(1)
             if live(n + 3):
                 square(n + 3, 1)
-            if live(n + 5):
-                regroup_x(n + 5)
+            if live(n + 6):
+                regroup_x(n + 6)
             if live(n + 4):
                 first_matmul(n + 4, 0)
                 square(n + 4, 0)

@@ -29,7 +29,7 @@ GROUPS = TOKENS // (P * GROUP_TILES)
 ROUND_TILES = 2
 ROUNDS = TOKENS // (P * ROUND_TILES)
 COLS = ROUND_TILES * P
-VECTOR_ROUNDS = 2
+VECTOR_ROUNDS = 1
 
 FLOPS = 2 * TOKENS * K * K + 2 * TOKENS * K * (HEADS * KV * HEAD)
 
@@ -74,14 +74,18 @@ def tile_mla_pa_t_kernel(
             nc.sync.dma_start(out=x_sb[:, g, cols], in_=x_groups[g][:, cols])
 
         wa_rows = wkv_a_w.rearrange("(p j) d -> p j d", j=PACK)
-        for b in range(2):
+
+        def load_wa(b):
             nc.sync.dma_start(out=wa_sb[:, block(b, 2), :], in_=wa_rows[:, block(b, 2), :])
+
         wb_heads = wkv_b_w.rearrange("(h s p) r -> h p s r", s=KV, p=P)
 
         def load_wb(h):
             nc.sync.dma_start(out=wb_sb[:, h], in_=wb_heads[h])
 
+        load_wa(0)
         load_x(0, 0)
+        load_wa(1)
         load_x(0, 1)
         nc.sync.dma_start(out=bias_a_bf[:], in_=wkv_a_b.rearrange("(p j) -> p j", j=PACK))
         nc.sync.dma_start(out=gain_bf[:], in_=kv_norm_w.rearrange("(p j) -> p j", j=PACK))
@@ -129,17 +133,21 @@ def tile_mla_pa_t_kernel(
         wa_grouped = keep.tile([P, K, PACK], BF16, align_bytes=64)
         wa_codes = keep.tile([P, K], U32, align_bytes=256)
         wa_scales = keep.tile([P, K], U8, align_bytes=256)
-        for b in range(2):
-            wa_bank = psum_o.tile([P, 2, WORDS, P], F32, tag="o")
-            transpose_words(wa_bank, [wa_sb[:, 2 * b + s, :] for s in range(2)])
-            copy = nc.vector.tensor_copy if b == 1 else nc.scalar.copy
-            copy(
+        wa_bank = {}
+
+        def transpose_wa(b):
+            wa_bank[b] = psum_o.tile([P, 2, WORDS, P], F32, tag="o", name="wa_bank")
+            transpose_words(wa_bank[b], [wa_sb[:, 2 * b + s, :] for s in range(2)])
+
+        def regroup_wa(b):
+            nc.scalar.copy(
                 out=wa_grouped[:, block(b, 2 * P), :]
                 .bitcast(F32)
                 .rearrange("p (s m) u -> p s m u", s=2),
-                in_=pair_words(wa_bank),
+                in_=pair_words(wa_bank[b]),
             )
-        for b in range(2):
+
+        def quantise_wa(b):
             nc.vector.quantize_mx(
                 out=wa_codes[:, block(b, 2 * P)].bitcast(FP8X4),
                 scales=wa_scales[:, block(b, 2 * P)],
@@ -149,9 +157,13 @@ def tile_mla_pa_t_kernel(
         bias_a = keep.tile([P, PACK], F32)
         gain = keep.tile([P, PACK], F32)
         gained_bias = keep.tile([P, PACK], F32)
-        nc.vector.tensor_copy(out=bias_a[:], in_=bias_a_bf[:])
-        nc.vector.tensor_copy(out=gain[:], in_=gain_bf[:])
-        nc.vector.tensor_tensor(out=gained_bias[:], in0=bias_a[:], in1=gain[:], op=MULT)
+
+        def widen_vectors():
+            nc.vector.tensor_copy(out=bias_a[:], in_=bias_a_bf[:])
+            nc.vector.tensor_copy(out=gain[:], in_=gain_bf[:])
+
+        def multiply_vectors():
+            nc.vector.tensor_tensor(out=gained_bias[:], in0=bias_a[:], in1=gain[:], op=MULT)
 
         wb_codes = keep.tile([P, KV, HEADS, HEAD], U32, align_bytes=256)
         wb_scales = keep.tile([P, KV, HEADS, HEAD], U8, align_bytes=256)
@@ -165,8 +177,7 @@ def tile_mla_pa_t_kernel(
 
         def regroup_wb(h):
             wb_grouped[h] = work.tile([P, KV, HEAD, PACK], BF16, align_bytes=64, name="wb_grouped")
-            copy = nc.vector.tensor_copy if h % 3 == 0 else nc.scalar.copy
-            copy(out=wb_grouped[h][:].bitcast(F32), in_=pair_words(wb_banks[h]))
+            nc.vector.tensor_copy(out=wb_grouped[h][:].bitcast(F32), in_=pair_words(wb_banks[h]))
 
         def quantise_wb(h):
             for s in range(KV):
@@ -289,16 +300,17 @@ def tile_mla_pa_t_kernel(
                 bias=eps[:],
             )
 
-        def normalise(r):
-            l_grouped[r] = latent.tile([P, COLS, PACK], BF16, align_bytes=64, name="l_grouped")
-            engine = nc.vector if r < VECTOR_ROUNDS else nc.gpsimd
+        def normalise(r, engine, first=0, count=ROUND_TILES):
+            if r not in l_grouped:
+                l_grouped[r] = latent.tile([P, COLS, PACK], BF16, align_bytes=64, name="l_grouped")
+            cols = slice(first * P, (first + count) * P)
             engine.tensor_tensor(
-                out=l_grouped[r][:].rearrange("p (c i) j -> p c j i", i=RUN),
-                in0=y[r][:].rearrange("p j (c i) -> p c j i", i=RUN),
-                in1=factor[r][:]
+                out=l_grouped[r][:, cols, :].rearrange("p (c i) j -> p c j i", i=RUN),
+                in0=y[r][:, :, cols].rearrange("p j (c i) -> p c j i", i=RUN),
+                in1=factor[r][:, cols]
                 .rearrange("p (c i) -> p c i", i=RUN)
                 .unsqueeze(2)
-                .to_broadcast([P, COLS // RUN, PACK, RUN]),
+                .to_broadcast([P, count * P // RUN, PACK, RUN]),
                 op=MULT,
             )
 
@@ -325,7 +337,7 @@ def tile_mla_pa_t_kernel(
                 )
 
         def add_second_bias(r, s, kv):
-            if s == 0 and kv == 0:
+            if r not in result:
                 result[r] = stage.tile([P, KV, ROUND_TILES, HEADS, HEAD], F32, name="result")
             for heads in ((slice(0, 2), slice(2, 4)) if (r, s, kv) == (ROUNDS - 1, 1, 1) else (slice(0, 4),)):
                 nc.vector.tensor_tensor(
@@ -334,6 +346,18 @@ def tile_mla_pa_t_kernel(
                     in1=bias_b_all[:, heads, kv, :],
                     op=ADD,
                 )
+
+        def add_second_bias_aside(r, s, kv):
+            if r not in result:
+                result[r] = stage.tile([P, KV, ROUND_TILES, HEADS, HEAD], F32, name="result")
+            plain = work.tile([P, HEADS, HEAD], F32, name="plain")
+            nc.scalar.copy(out=plain[:], in_=o_bank[r, s, kv][:])
+            nc.gpsimd.tensor_tensor(
+                out=result[r][:, kv, s],
+                in0=plain[:],
+                in1=bias_b_all[:, :, kv, :],
+                op=ADD,
+            )
 
         def store(r, kv, first=0, count=ROUND_TILES):
             g, tile = divmod(r * ROUND_TILES + first, GROUP_TILES)
@@ -351,58 +375,153 @@ def tile_mla_pa_t_kernel(
             transpose_wb(h)
             regroup_wb(h)
 
-        for n in range(-6, ROUNDS + 1):
+        done = set()
+
+        def once(step, *where):
+            if (step, where) not in done:
+                done.add((step, where))
+                step(*where)
+
+        transpose_wa(0)
+        once(transpose_x, 0)
+        transpose_wa(1)
+        once(transpose_x, 1)
+        regroup_wa(0)
+        once(regroup_x, 0)
+        regroup_wa(1)
+        once(regroup_x, 1)
+        quantise_wa(0)
+        widen_vectors()
+        once(quantise_x, 0)
+        quantise_wa(1)
+        multiply_vectors()
+        once(quantise_x, 1)
+        once(first_matmul, 0, 0)
+        once(first_matmul, 0, 1)
+        once(transpose_x, 2)
+        once(transpose_wb, 0)
+        once(transpose_wb, 1)
+        once(square, 0, 0)
+        once(square, 0, 1)
+        once(regroup_x, 2)
+        once(bias_and_gain, 0, 0)
+        once(bias_and_gain, 0, 1)
+        once(regroup_wb, 0)
+        once(quantise_x, 2)
+        once(first_matmul, 1, 0)
+        once(first_matmul, 1, 1)
+        once(add_squares, 0)
+        once(transpose_wb, 2)
+        once(transpose_x, 3)
+        once(square, 1, 0)
+        once(square, 1, 1)
+        once(quantise_wb, 0)
+        once(sum_features, 0)
+        once(regroup_wb, 1)
+        once(spread_sums, 0)
+        once(transpose_wb, 3)
+        once(quantise_wb, 1)
+        once(regroup_wb, 2)
+        once(bias_and_gain, 1, 0)
+        once(bias_and_gain, 1, 1)
+        once(inverse_root, 0)
+        once(normalise, 0, nc.vector)
+        once(regroup_x, 3)
+        once(transpose_x, 4)
+        once(first_matmul, 2, 0)
+        once(first_matmul, 2, 1)
+        once(add_squares, 1)
+        once(square, 2, 0)
+        once(square, 2, 1)
+        once(quantise_wb, 2)
+        once(regroup_wb, 3)
+        once(quantise_latent, 0)
+        once(sum_features, 1)
+        once(quantise_x, 3)
+        once(quantise_wb, 3)
+        for n in range(-3, ROUNDS - 1):
+            if live(n):
+                once(square, n, 0)
+                once(square, n, 1)
             if live(n - 1):
-                second_matmul(n - 1, 1)
-                for kv in range(KV):
-                    add_second_bias(n - 1, 1, kv)
-                    if n - 1 >= ROUNDS - 2:
-                        store(n - 1, kv, 1, 1)
-                    else:
-                        store(n - 1, kv)
-            if n == -3:
-                quantise_wb(1)
-                prepare_wb(2)
-            if live(n + 2):
-                add_squares(n + 2)
-                sum_features(n + 2)
+                once(spread_sums, n - 1)
             if live(n + 3):
-                first_matmul(n + 3, 1)
-            if live(n + 3):
-                bias_and_gain(n + 3, 0)
-                bias_and_gain(n + 3, 1)
+                once(transpose_x, n + 3)
             if live(n):
-                second_matmul(n, 0)
-                add_second_bias(n, 0, 0)
-            if n == -4:
-                prepare_wb(0)
+                once(add_squares, n)
+                once(bias_and_gain, n, 0)
+            if live(n - 2):
+                once(quantise_latent, n - 2)
+            if live(n + 2):
+                once(quantise_x, n + 2)
+            if live(n - 1):
+                once(inverse_root, n - 1)
+                if n - 1 >= VECTOR_ROUNDS:
+                    normalise(n - 1, nc.gpsimd)
+            if live(n):
+                once(bias_and_gain, n, 1)
+            if live(n + 3):
+                once(regroup_x, n + 3)
+            if live(n):
+                once(sum_features, n)
             if live(n + 1):
-                quantise_latent(n + 1)
-            if live(n + 5):
-                quantise_x(n + 5)
-            if n == -3:
-                quantise_wb(2)
-                prepare_wb(3)
-            if live(n + 2):
-                spread_sums(n + 2)
-                inverse_root(n + 2)
-                normalise(n + 2)
-            if live(n + 6):
-                transpose_x(n + 6)
-            if live(n):
-                add_second_bias(n, 0, 1)
-                if n >= ROUNDS - 2:
+                once(first_matmul, n + 1, 0)
+            if live(n - 2):
+                once(second_matmul, n - 2, 0)
+            if live(n + 1):
+                once(first_matmul, n + 1, 1)
+            if live(n - 2):
+                once(second_matmul, n - 2, 1)
+                for s in range(ROUND_TILES):
                     for kv in range(KV):
-                        store(n, kv, 0, 1)
-            if n == -4:
-                quantise_wb(0)
-                prepare_wb(1)
-            if live(n + 3):
-                square(n + 3, 1)
-            if live(n + 6):
-                regroup_x(n + 6)
-            if live(n + 4):
-                first_matmul(n + 4, 0)
-                square(n + 4, 0)
-            if n == -3:
-                quantise_wb(3)
+                        once(add_second_bias, n - 2, s, kv)
+                        if n - 2 >= ROUNDS - 2:
+                            store(n - 2, kv, s, 1)
+                        elif s == 1:
+                            once(store, n - 2, kv)
+        once(square, 15, 0)
+        once(square, 15, 1)
+        once(spread_sums, 14)
+        once(add_squares, 15)
+        once(bias_and_gain, 15, 0)
+        once(quantise_latent, 13)
+        once(inverse_root, 14)
+        normalise(14, nc.gpsimd)
+        once(bias_and_gain, 15, 1)
+        once(sum_features, 15)
+        once(second_matmul, 13, 0)
+        once(spread_sums, 15)
+        once(second_matmul, 13, 1)
+        once(add_second_bias, 13, 0, 0)
+        store(13, 0, 0, 1)
+        once(add_second_bias, 13, 0, 1)
+        store(13, 1, 0, 1)
+        once(inverse_root, 15)
+        normalise(15, nc.vector, 1, 1)
+        once(quantise_latent, 14)
+        normalise(15, nc.gpsimd, 0, 1)
+        once(add_second_bias, 13, 1, 0)
+        store(13, 0, 1, 1)
+        once(add_second_bias, 13, 1, 1)
+        store(13, 1, 1, 1)
+        once(second_matmul, 14, 0)
+        once(add_second_bias, 14, 0, 0)
+        store(14, 0, 0, 1)
+        once(add_second_bias, 14, 0, 1)
+        store(14, 1, 0, 1)
+        once(quantise_latent, 15)
+        once(second_matmul, 14, 1)
+        once(add_second_bias, 14, 1, 0)
+        store(14, 0, 1, 1)
+        once(add_second_bias, 14, 1, 1)
+        store(14, 1, 1, 1)
+        once(second_matmul, 15, 0)
+        once(add_second_bias, 15, 0, 0)
+        store(15, 0, 0, 1)
+        once(add_second_bias, 15, 0, 1)
+        store(15, 1, 0, 1)
+        once(second_matmul, 15, 1)
+        once(add_second_bias, 15, 1, 0)
+        store(15, 0, 1, 1)
+        once(add_second_bias, 15, 1, 1)
+        store(15, 1, 1, 1)

@@ -246,7 +246,7 @@ def tile_mla_pa_t_kernel(
                 y[r] = work.tile([P, PACK, COLS], F32, name="y")
             for e in range(2):
                 j = 2 * half + e
-                if r < VECTOR_ROUNDS:
+                if r < VECTOR_ROUNDS or (j == PACK - 1 and r > 2):
                     nc.vector.tensor_scalar(
                         out=y[r][:, j, :],
                         in0=c_bank[r, half][:, e, :],

@@ -55,7 +55,7 @@ def tile_mla_pa_t_kernel(
     with ExitStack() as stack:
         keep = stack.enter_context(tc.tile_pool(name="keep", bufs=1))
         work = stack.enter_context(tc.tile_pool(name="work", bufs=4))
-        latent = stack.enter_context(tc.tile_pool(name="latent", bufs=2))
+        latent = stack.enter_context(tc.tile_pool(name="latent", bufs=1))
         stage = stack.enter_context(tc.tile_pool(name="stage", bufs=12))
         psum_c = stack.enter_context(tc.psum_pool(name="psum_c", bufs=1))
         psum_s = stack.enter_context(tc.psum_pool(name="psum_s", bufs=1))
@@ -443,10 +443,10 @@ def tile_mla_pa_t_kernel(
             if live(n):
                 once(square, n, 0)
                 once(square, n, 1)
-            if live(n - 1):
-                once(spread_sums, n - 1)
             if live(n + 3):
                 once(transpose_x, n + 3)
+            if live(n - 1):
+                once(spread_sums, n - 1)
             if live(n):
                 once(add_squares, n)
                 once(bias_and_gain, n, 0)
@@ -497,22 +497,22 @@ def tile_mla_pa_t_kernel(
         once(add_second_bias, 13, 0, 1)
         store(13, 1, 0, 1)
         once(inverse_root, 15)
-        normalise(15, nc.vector, 1, 1)
-        once(quantise_latent, 14)
-        normalise(15, nc.gpsimd, 0, 1)
         once(add_second_bias, 13, 1, 0)
         store(13, 0, 1, 1)
         once(add_second_bias, 13, 1, 1)
         store(13, 1, 1, 1)
+        once(quantise_latent, 14)
+        normalise(15, nc.vector, 1, 1)
+        normalise(15, nc.gpsimd, 0, 1)
         once(second_matmul, 14, 0)
         once(add_second_bias, 14, 0, 0)
         store(14, 0, 0, 1)
         once(add_second_bias, 14, 0, 1)
         store(14, 1, 0, 1)
-        once(quantise_latent, 15)
         once(second_matmul, 14, 1)
         once(add_second_bias, 14, 1, 0)
         store(14, 0, 1, 1)
+        once(quantise_latent, 15)
         once(add_second_bias, 14, 1, 1)
         store(14, 1, 1, 1)
         once(second_matmul, 15, 0)

from contextlib import ExitStack

import concourse.mybir as mybir
from concourse.masks import make_identity

F32 = mybir.dt.float32
BF16 = mybir.dt.bfloat16
U32 = mybir.dt.uint32
U8 = mybir.dt.uint8
FP8X4 = mybir.dt.float8_e4m3fn_x4
ADD = mybir.AluOpType.add
MULT = mybir.AluOpType.mult
ACT = mybir.ActivationFunctionType
AXIS_X = mybir.AxisListType.X

P = 128
PACK = 4
WORDS = 2
TOKENS = 4096
K = 512
HEADS = 4
HEAD = 128
KV = 2
EPS = 1e-6
RUN = 4

GROUP_TILES = 4
GROUPS = TOKENS // (P * GROUP_TILES)
ROUND_TILES = 2
ROUNDS = TOKENS // (P * ROUND_TILES)
COLS = ROUND_TILES * P
VECTOR_ROUNDS = 1

FLOPS = 2 * TOKENS * K * K + 2 * TOKENS * K * (HEADS * KV * HEAD)


def block(i, width):
    return slice(i * width, (i + 1) * width)


def live(r):
    return 0 <= r < ROUNDS


def tile_mla_pa_t_kernel(
    tc, x, wkv_a_w, wkv_a_b, kv_norm_w, wkv_b_w, wkv_b_b, out_0, out_1
):
    nc = tc.nc
    x_groups = x.flatten_outer_dims().rearrange("(g p i) d -> g p (i d)", p=P, i=GROUP_TILES)
    out_groups = [
        o.rearrange("b s h c -> (b s) (h c)").rearrange("(g p i) n -> g p i n", p=P, i=GROUP_TILES)
        for o in (out_0, out_1)
    ]

    with ExitStack() as stack:
        keep = stack.enter_context(tc.tile_pool(name="keep", bufs=1))
        work = stack.enter_context(tc.tile_pool(name="work", bufs=4))
        latent = stack.enter_context(tc.tile_pool(name="latent", bufs=1))
        stage = stack.enter_context(tc.tile_pool(name="stage", bufs=12))
        psum_c = stack.enter_context(tc.psum_pool(name="psum_c", bufs=1))
        psum_s = stack.enter_context(tc.psum_pool(name="psum_s", bufs=1))
        psum_o = stack.enter_context(tc.psum_pool(name="psum_o", bufs=4))
        stack.enter_context(tc.manual_schedule())

        bias_a_bf = keep.tile([P, PACK], BF16)
        gain_bf = keep.tile([P, PACK], BF16)
        bias_b_all = keep.tile([P, HEADS, KV, HEAD], BF16)
        wa_sb = keep.tile([P, PACK, K], BF16)
        wb_sb = keep.tile([P, HEADS, KV, K], BF16)
        x_sb = keep.tile([P, GROUPS, GROUP_TILES * K], BF16)

        def load_x(g, half):
            cols = block(half, ROUND_TILES * K)
            nc.sync.dma_start(out=x_sb[:, g, cols], in_=x_groups[g][:, cols])

        wa_rows = wkv_a_w.rearrange("(p j) d -> p j d", j=PACK)

        def load_wa(b):
            nc.sync.dma_start(out=wa_sb[:, block(b, 2), :], in_=wa_rows[:, block(b, 2), :])

        wb_heads = wkv_b_w.rearrange("(h s p) r -> h p s r", s=KV, p=P)

        def load_wb(h):
            nc.sync.dma_start(out=wb_sb[:, h], in_=wb_heads[h])

        load_wa(0)
        load_x(0, 0)
        load_wa(1)
        load_x(0, 1)
        nc.sync.dma_start(out=bias_a_bf[:], in_=wkv_a_b.rearrange("(p j) -> p j", j=PACK))
        nc.sync.dma_start(out=gain_bf[:], in_=kv_norm_w.rearrange("(p j) -> p j", j=PACK))
        load_wb(0)
        load_x(1, 0)
        load_wb(1)
        load_x(1, 1)
        load_wb(2)
        load_wb(3)
        for g in range(2, GROUPS):
            nc.sync.dma_start(out=x_sb[:, g, :], in_=x_groups[g])
            if g == 3:
                nc.sync.dma_start(
                    out=bias_b_all[:].rearrange("p h s c -> p (h s c)"),
                    in_=wkv_b_b.partition_broadcast(P),
                )

        zeros = keep.tile([P, K], BF16)
        nc.vector.memset(zeros[:], 0.0)
        ident = keep.tile([P, P], F32)
        make_identity(nc, ident[:])
        eps = keep.tile([P, 1], F32)
        nc.vector.memset(eps[:], 0.0)
        nc.vector.tensor_scalar(out=eps[:], in0=eps[:], scalar1=EPS, scalar2=None, op0=ADD)
        one = keep.tile([P, 1], F32)
        nc.vector.memset(one[:], 1.0)
        nc.scalar.activation(out=one[:], in_=one[:], func=ACT.Abs_reciprocal_sqrt)

        def keep_warm(count):
            bank = psum_s.tile([P, K], F32, tag="q", name="warm_bank")
            for i in range(count):
                nc.tensor.matmul(out=bank[:], lhsT=zeros[:, 0:P], rhs=zeros[:], start=True, stop=True)

        keep_warm(4)

        def transpose_words(bank, rows):
            for s in range(len(rows)):
                words = rows[s].bitcast(F32)
                for u in range(WORDS):
                    nc.tensor.transpose(bank[:, s, u, :], words[:, u::WORDS], ident[:])

        def pair_words(bank):
            return bank[:].rearrange("p s u m -> p s m u")

        wa_grouped = keep.tile([P, K, PACK], BF16, align_bytes=64)
        wa_codes = keep.tile([P, K], U32, align_bytes=256)
        wa_scales = keep.tile([P, K], U8, align_bytes=256)
        wa_bank = {}

        def transpose_wa(b):
            wa_bank[b] = psum_o.tile([P, 2, WORDS, P], F32, tag="o", name="wa_bank")
            transpose_words(wa_bank[b], [wa_sb[:, 2 * b + s, :] for s in range(2)])

        def regroup_wa(b):
            nc.scalar.copy(
                out=wa_grouped[:, block(b, 2 * P), :]
                .bitcast(F32)
                .rearrange("p (s m) u -> p s m u", s=2),
                in_=pair_words(wa_bank[b]),
            )

        def quantise_wa(b):
            nc.vector.quantize_mx(
                out=wa_codes[:, block(b, 2 * P)].bitcast(FP8X4),
                scales=wa_scales[:, block(b, 2 * P)],
                in_=wa_grouped[:, block(b, 2 * P), :].rearrange("p m j -> p (m j)"),
            )

        bias_a = keep.tile([P, PACK], F32)
        gain = keep.tile([P, PACK], F32)
        gained_bias = keep.tile([P, PACK], F32)

        def widen_vectors():
            nc.vector.tensor_copy(out=bias_a[:], in_=bias_a_bf[:])
            nc.vector.tensor_copy(out=gain[:], in_=gain_bf[:])

        def multiply_vectors():
            nc.vector.tensor_tensor(out=gained_bias[:], in0=bias_a[:], in1=gain[:], op=MULT)

        wb_codes = keep.tile([P, KV, HEADS, HEAD], U32, align_bytes=256)
        wb_scales = keep.tile([P, KV, HEADS, HEAD], U8, align_bytes=256)
        wb_banks = {}

        def transpose_wb(h):
            wb_banks[h] = psum_o.tile([P, KV, WORDS, P], F32, tag="o", name="wb_bank")
            transpose_words(wb_banks[h], [wb_sb[:, h, s, :] for s in range(KV)])

        wb_grouped = {}

        def regroup_wb(h):
            wb_grouped[h] = work.tile([P, KV, HEAD, PACK], BF16, align_bytes=64, name="wb_grouped")
            nc.vector.tensor_copy(out=wb_grouped[h][:].bitcast(F32), in_=pair_words(wb_banks[h]))

        def quantise_wb(h):
            for s in range(KV):
                nc.vector.quantize_mx(
                    out=wb_codes[:, s, h, :].bitcast(FP8X4),
                    scales=wb_scales[:, s, h, :],
                    in_=wb_grouped[h][:, s].rearrange("p m j -> p (m j)"),
                )

        x_bank, x_grouped, x_codes, x_scales = {}, {}, {}, {}
        c_bank, y, squares, q_bank, sum_sq = {}, {}, {}, {}, {}
        factor_bank, factor = {}, {}
        l_grouped, l_codes, l_scales = {}, {}, {}
        o_bank, result = {}, {}

        def transpose_x(r):
            g, first = divmod(r * ROUND_TILES, GROUP_TILES)
            x_bank[r] = psum_o.tile([P, ROUND_TILES, WORDS, P], F32, tag="o", name="x_bank")
            transpose_words(
                x_bank[r], [x_sb[:, g, block(first + s, K)] for s in range(ROUND_TILES)]
            )

        def regroup_x(r):
            x_grouped[r] = work.tile(
                [P, ROUND_TILES, P, PACK], BF16, align_bytes=64, name="x_grouped"
            )
            nc.scalar.copy(out=x_grouped[r][:].bitcast(F32), in_=pair_words(x_bank[r]))

        def quantise_x(r):
            x_codes[r] = work.tile([P, COLS], U32, align_bytes=256, name="x_codes")
            x_scales[r] = work.tile([P, COLS], U8, align_bytes=256, name="x_scales")
            nc.vector.quantize_mx(
                out=x_codes[r][:].bitcast(FP8X4),
                scales=x_scales[r][:],
                in_=x_grouped[r][:].rearrange("p s m j -> p (s m j)"),
            )

        def first_matmul(r, half):
            c_bank[r, half] = psum_c.tile([P, 2, COLS], F32, tag="c%d" % half, name="c_bank")
            for e in range(2):
                j = 2 * half + e
                nc.tensor.matmul_mx(
                    out=c_bank[r, half][:, e, :],
                    lhsT=wa_codes[:, block(j, P)].bitcast(FP8X4),
                    lhsT_scale=wa_scales[:, block(j, P)],
                    rhs=x_codes[r][:].bitcast(FP8X4),
                    rhs_scale=x_scales[r][:],
                    start=True,
                    stop=True,
                )

        def square(r, half):
            if r not in squares:
                squares[r] = work.tile([P, PACK, COLS], F32, name="squares")
            for e in range(2):
                j = 2 * half + e
                nc.scalar.activation(
                    out=squares[r][:, j, :],
                    in_=c_bank[r, half][:, e, :],
                    func=ACT.Square,
                    bias=bias_a[:, j : j + 1],
                )

        def bias_and_gain(r, half):
            if r not in y:
                y[r] = work.tile([P, PACK, COLS], F32, name="y")
            for e in range(2):
                j = 2 * half + e
                if r < VECTOR_ROUNDS or (j == PACK - 1 and r > 2):
                    nc.vector.tensor_scalar(
                        out=y[r][:, j, :],
                        in0=c_bank[r, half][:, e, :],
                        scalar1=bias_a[:, j : j + 1],
                        scalar2=gain[:, j : j + 1],
                        op0=ADD,
                        op1=MULT,
                    )
                else:
                    nc.scalar.activation(
                        out=y[r][:, j, :],
                        in_=c_bank[r, half][:, e, :],
                        func=ACT.Identity,
                        scale=gain[:, j : j + 1],
                        bias=gained_bias[:, j : j + 1],
                    )

        def add_squares(r):
            q_bank[r] = psum_s.tile([P, ROUND_TILES, P], F32, tag="q", name="q_bank")
            for s in range(ROUND_TILES):
                for j in range(PACK):
                    nc.tensor.matmul(
                        out=q_bank[r][:, s, :],
                        lhsT=squares[r][:, j, block(s, P)],
                        rhs=ident[:],
                        is_transpose=True,
                        start=(j == 0),
                        stop=(j == PACK - 1),
                    )

        def sum_features(r):
            sum_sq[r] = work.tile([P, ROUND_TILES], F32, name="sum_sq")
            nc.vector.tensor_reduce(out=sum_sq[r][:], in_=q_bank[r][:], op=ADD, axis=AXIS_X)

        def spread_sums(r):
            factor_bank[r] = psum_s.tile([P, ROUND_TILES, P], F32, tag="f", name="factor_bank")
            for s in range(ROUND_TILES):
                nc.tensor.transpose(
                    factor_bank[r][:, s, :],
                    sum_sq[r][:, s : s + 1].to_broadcast([P, P]),
                    ident[:],
                )

        def inverse_root(r):
            factor[r] = work.tile([P, COLS], F32, name="factor")
            nc.scalar.activation(
                out=factor[r][:],
                in_=factor_bank[r][:].rearrange("p s m -> p (s m)"),
                func=ACT.Abs_reciprocal_sqrt,
                scale=1.0 / K,
                bias=eps[:],
            )

        def normalise(r, engine, first=0, count=ROUND_TILES):
            if r not in l_grouped:
                l_grouped[r] = latent.tile([P, COLS, PACK], BF16, align_bytes=64, name="l_grouped")
            cols = slice(first * P, (first + count) * P)
            engine.tensor_tensor(
                out=l_grouped[r][:, cols, :].rearrange("p (c i) j -> p c j i", i=RUN),
                in0=y[r][:, :, cols].rearrange("p j (c i) -> p c j i", i=RUN),
                in1=factor[r][:, cols]
                .rearrange("p (c i) -> p c i", i=RUN)
                .unsqueeze(2)
                .to_broadcast([P, count * P // RUN, PACK, RUN]),
                op=MULT,
            )

        def quantise_latent(r):
            l_codes[r] = work.tile([P, COLS], U32, align_bytes=256, name="l_codes")
            l_scales[r] = work.tile([P, COLS], U8, align_bytes=256, name="l_scales")
            nc.vector.quantize_mx(
                out=l_codes[r][:].bitcast(FP8X4),
                scales=l_scales[r][:],
                in_=l_grouped[r][:].rearrange("p m j -> p (m j)"),
            )

        def second_matmul(r, s):
            for kv in range(KV):
                o_bank[r, s, kv] = psum_o.tile([P, HEADS, HEAD], F32, tag="o", name="o_bank")
                nc.tensor.matmul_mx(
                    out=o_bank[r, s, kv][:].rearrange("p h c -> p (h c)"),
                    lhsT=l_codes[r][:, block(s, P)].bitcast(FP8X4),
                    lhsT_scale=l_scales[r][:, block(s, P)],
                    rhs=wb_codes[:, kv].rearrange("p h c -> p (h c)").bitcast(FP8X4),
                    rhs_scale=wb_scales[:, kv].rearrange("p h c -> p (h c)"),
                    start=True,
                    stop=True,
                )

        def add_second_bias(r, s, kv):
            if r not in result:
                result[r] = stage.tile([P, KV, ROUND_TILES, HEADS, HEAD], F32, name="result")
            for heads in ((slice(0, 2), slice(2, 4)) if (r, s, kv) == (ROUNDS - 1, 1, 1) else (slice(0, 4),)):
                nc.vector.tensor_tensor(
                    out=result[r][:, kv, s, heads],
                    in0=o_bank[r, s, kv][:, heads],
                    in1=bias_b_all[:, heads, kv, :],
                    op=ADD,
                )

        def add_second_bias_aside(r, s, kv):
            if r not in result:
                result[r] = stage.tile([P, KV, ROUND_TILES, HEADS, HEAD], F32, name="result")
            plain = work.tile([P, HEADS, HEAD], F32, name="plain")
            nc.scalar.copy(out=plain[:], in_=o_bank[r, s, kv][:])
            nc.gpsimd.tensor_tensor(
                out=result[r][:, kv, s],
                in0=plain[:],
                in1=bias_b_all[:, :, kv, :],
                op=ADD,
            )

        def store(r, kv, first=0, count=ROUND_TILES):
            g, tile = divmod(r * ROUND_TILES + first, GROUP_TILES)
            for heads in ((slice(0, 2), slice(2, 4)) if (r, first, kv) == (ROUNDS - 1, 1, 1) else (slice(0, 4),)):
                nc.sync.dma_start(
                    out=out_groups[kv][g][
                        :, tile : tile + count, heads.start * HEAD : heads.stop * HEAD
                    ],
                    in_=result[r][:, kv, first : first + count, heads].rearrange(
                        "p s h c -> p s (h c)"
                    ),
                )

        def prepare_wb(h):
            transpose_wb(h)
            regroup_wb(h)

        done = set()

        def once(step, *where):
            if (step, where) not in done:
                done.add((step, where))
                step(*where)

        transpose_wa(0)
        once(transpose_x, 0)
        transpose_wa(1)
        once(transpose_x, 1)
        regroup_wa(0)
        once(regroup_x, 0)
        regroup_wa(1)
        once(regroup_x, 1)
        quantise_wa(0)
        widen_vectors()
        once(quantise_x, 0)
        quantise_wa(1)
        multiply_vectors()
        once(quantise_x, 1)
        once(first_matmul, 0, 0)
        once(first_matmul, 0, 1)
        once(transpose_x, 2)
        once(transpose_wb, 0)
        once(transpose_wb, 1)
        once(square, 0, 0)
        once(square, 0, 1)
        once(regroup_x, 2)
        once(bias_and_gain, 0, 0)
        once(bias_and_gain, 0, 1)
        once(regroup_wb, 0)
        once(quantise_x, 2)
        once(first_matmul, 1, 0)
        once(first_matmul, 1, 1)
        once(add_squares, 0)
        once(transpose_wb, 2)
        once(transpose_x, 3)
        once(square, 1, 0)
        once(square, 1, 1)
        once(quantise_wb, 0)
        once(sum_features, 0)
        once(regroup_wb, 1)
        once(spread_sums, 0)
        once(transpose_wb, 3)
        once(quantise_wb, 1)
        once(regroup_wb, 2)
        once(bias_and_gain, 1, 0)
        once(bias_and_gain, 1, 1)
        once(inverse_root, 0)
        once(normalise, 0, nc.vector)
        once(regroup_x, 3)
        once(transpose_x, 4)
        once(first_matmul, 2, 0)
        once(first_matmul, 2, 1)
        once(add_squares, 1)
        once(square, 2, 0)
        once(square, 2, 1)
        once(quantise_wb, 2)
        once(regroup_wb, 3)
        once(quantise_latent, 0)
        once(sum_features, 1)
        once(quantise_x, 3)
        once(quantise_wb, 3)
        for n in range(-3, ROUNDS - 1):
            if live(n):
                once(square, n, 0)
                once(square, n, 1)
            if live(n + 3):
                once(transpose_x, n + 3)
            if live(n - 1):
                once(spread_sums, n - 1)
            if live(n):
                once(add_squares, n)
                once(bias_and_gain, n, 0)
            if live(n - 2):
                once(quantise_latent, n - 2)
            if live(n + 2):
                once(quantise_x, n + 2)
            if live(n - 1):
                once(inverse_root, n - 1)
                if n - 1 >= VECTOR_ROUNDS:
                    normalise(n - 1, nc.gpsimd)
            if live(n):
                once(bias_and_gain, n, 1)
            if live(n + 3):
                once(regroup_x, n + 3)
            if live(n):
                once(sum_features, n)
            if live(n + 1):
                once(first_matmul, n + 1, 0)
            if live(n - 2):
                once(second_matmul, n - 2, 0)
            if live(n + 1):
                once(first_matmul, n + 1, 1)
            if live(n - 2):
                once(second_matmul, n - 2, 1)
                for s in range(ROUND_TILES):
                    for kv in range(KV):
                        once(add_second_bias, n - 2, s, kv)
                        if n - 2 >= ROUNDS - 2:
                            store(n - 2, kv, s, 1)
                        elif s == 1:
                            once(store, n - 2, kv)
        once(square, 15, 0)
        once(square, 15, 1)
        once(spread_sums, 14)
        once(add_squares, 15)
        once(bias_and_gain, 15, 0)
        once(quantise_latent, 13)
        once(inverse_root, 14)
        normalise(14, nc.gpsimd)
        once(bias_and_gain, 15, 1)
        once(sum_features, 15)
        once(second_matmul, 13, 0)
        once(spread_sums, 15)
        once(second_matmul, 13, 1)
        once(add_second_bias, 13, 0, 0)
        store(13, 0, 0, 1)
        once(add_second_bias, 13, 0, 1)
        store(13, 1, 0, 1)
        once(inverse_root, 15)
        once(add_second_bias, 13, 1, 0)
        store(13, 0, 1, 1)
        once(add_second_bias, 13, 1, 1)
        store(13, 1, 1, 1)
        once(quantise_latent, 14)
        normalise(15, nc.vector, 1, 1)
        normalise(15, nc.gpsimd, 0, 1)
        once(second_matmul, 14, 0)
        once(add_second_bias, 14, 0, 0)
        store(14, 0, 0, 1)
        once(add_second_bias, 14, 0, 1)
        store(14, 1, 0, 1)
        once(second_matmul, 14, 1)
        once(add_second_bias, 14, 1, 0)
        store(14, 0, 1, 1)
        once(quantise_latent, 15)
        once(add_second_bias, 14, 1, 1)
        store(14, 1, 1, 1)
        once(second_matmul, 15, 0)
        once(add_second_bias, 15, 0, 0)
        store(15, 0, 0, 1)
        once(add_second_bias, 15, 0, 1)
        store(15, 1, 0, 1)
        once(second_matmul, 15, 1)
        once(add_second_bias, 15, 1, 0)
        store(15, 0, 1, 1)
        once(add_second_bias, 15, 1, 1)
        store(15, 1, 1, 1)
